import numpy as np
import ml_dtypes


def mxq(x, axis, fmt="e4m3"):
    dtype, down = {"e4m3": (ml_dtypes.float8_e4m3fn, 7), "e5m2": (ml_dtypes.float8_e5m2, 14)}[fmt]
    v = np.moveaxis(np.asarray(x, np.float32).astype(ml_dtypes.bfloat16).astype(np.float64), axis, -1)
    blocks = v.reshape(v.shape[:-1] + (-1, 32))
    amax = np.abs(blocks).max(-1, keepdims=True)
    byte = np.maximum(np.where(amax > 0, np.frexp(amax)[1] - 1 + 127, 0) - down, 1)
    scale = np.exp2(byte - 127.0)
    codes = (blocks / scale).astype(np.float32).astype(dtype).astype(np.float64)
    return np.moveaxis((codes * scale).reshape(v.shape), -1, axis)


WIDE = False


def mx_kscale(k):
    if not WIDE:
        return np.ones(k)
    levels = np.array([10, -10, 5, -5, 0])
    a = np.random.permutation(np.resize(levels, k // 512 * 4)).reshape(k // 512, 4)
    idx = np.arange(k)
    return np.exp2(a[idx // 512, idx % 128 // 32])


BF16 = ml_dtypes.bfloat16


def bf(x):
    return np.asarray(x, np.float32).astype(BF16)


def f64(x):
    return np.asarray(x).astype(np.float64)


B, N, C, H = 2, 512, 512, 8
HD = C // H
ALPHA = 0.6
SIG = 2.0


def get_s(w):
    d = w.sum(-1) ** -0.5
    return np.swapaxes(w, -1, -2) * d[..., :, None] * d[..., None, :]


def merge(o):
    return o.transpose(0, 2, 1, 3).reshape(B, N, C)


def draw_map(t):
    e = np.exp(SIG * np.random.standard_normal((B, H, N, N))) * t
    rows = np.exp(0.5 * np.random.standard_normal((B, H, N, 1)))
    return bf(e / e.sum(-1, keepdims=True) * rows)


def setup_inputs():
    t = mx_kscale(N)
    t = t / t.max()
    return {"attn_r": draw_map(t), "attn_d": draw_map(t),
            "v_d": bf(np.random.standard_normal((B, H, N, HD)) * 1.4 / t[:, None])}


def reference(attn_r, attn_d, v_d):
    wr, wd, v = f64(attn_r), f64(attn_d), f64(v_d)
    sr = mxq(get_s(wr), 3, "e4m3")
    sd = mxq(get_s(wd), 3, "e4m3")
    p = sr @ sd.transpose(0, 1, 3, 2)
    a = ALPHA * p + (1.0 - ALPHA) * (wr + wd)
    vq = mxq(v, 2, "e4m3")
    out_rd = merge(mxq(a, 3, "e4m3") @ vq)
    out_d = merge(mxq(wd, 3, "e4m3") @ vq)
    return (out_rd, out_d)

@@ -1,0 +1,251 @@
+from contextlib import ExitStack
+
+import concourse.bass as bass
+import concourse.mybir as mybir
+import concourse.tile as tile
+from concourse.masks import make_identity
+
+F32 = mybir.dt.float32
+BF16 = mybir.dt.bfloat16
+U32 = mybir.dt.uint32
+U8 = mybir.dt.uint8
+FP8X4 = mybir.dt.float8_e4m3fn_x4
+ALU = mybir.AluOpType
+ACT = mybir.ActivationFunctionType
+
+P = 128
+N = 512
+HD = 64
+NB = 2
+NHB = 8
+NH = NB * NHB
+ALPHA = 0.6
+BETA = 0.4
+
+FLOPS = NH * (2 * N * N * N + 2 * 2 * N * N * HD)
+
+
+def tile_multiattention_pa_kernel(tc, attn_r, attn_d, v_d, out_rd, out_d):
+    nc = tc.nc
+    wr_v = attn_r.rearrange("b h (t p) n -> (b h) p t n", p=P)
+    wd_v = attn_d.rearrange("b h (t p) n -> (b h) p t n", p=P)
+    with ExitStack() as ctx:
+        const = ctx.enter_context(tc.tile_pool(name="const", bufs=1))
+        ld = ctx.enter_context(tc.tile_pool(name="ld", bufs=4))
+        wk = ctx.enter_context(tc.tile_pool(name="wk", bufs=2))
+        ps = ctx.enter_context(tc.psum_pool(name="ps", bufs=1))
+
+        ctx.enter_context(tc.manual_schedule())
+        ident = const.tile([P, P], F32, name="ident")
+        make_identity(nc, ident[:])
+
+        vcodes = {}
+        vscales = {}
+        st = {}
+
+        vraw = {}
+        vgrp = {}
+
+        def vload(key):
+            raw = const.tile([P, NH, 4, HD], BF16, name="vraw_" + key)
+            if key == "t":
+                nc.sync.dma_start(out=raw[:].rearrange("p g j d -> p (g j) d"),
+                                  in_=v_d.rearrange("b h (j p) d -> p (b h j) d", p=P))
+            else:
+                nc.sync.dma_start(out=raw[:].rearrange("p g (u e) d -> p (g u) (e d)", u=2),
+                                  in_=v_d.rearrange("b h (u p e) d -> p (b h u) (e d)", u=2, e=2))
+            vraw[key] = raw
+            vcodes[key] = const.tile([P, NH * HD], U32, name="vc_" + key, align_bytes=64)
+            vscales[key] = const.tile([P, NH * HD], U8, name="vs_" + key, align_bytes=64)
+
+        def vreg(key, b):
+            grp = const.tile([P, NHB, HD, 4], BF16, name="vgrp", tag="vgrp", bufs=2, align_bytes=64)
+            nc.gpsimd.tensor_scalar(out=grp[:], in0=vraw[key][:, NHB * b:NHB * b + NHB].rearrange("p g j d -> p g d j"),
+                                    scalar1=1.0, scalar2=0.0, op0=ALU.mult, op1=ALU.add)
+            vgrp[(key, b)] = grp
+
+        def q_v(key, b):
+            w = NHB * HD
+            nc.vector.quantize_mx(out=vcodes[key][:, w * b:w * b + w].bitcast(FP8X4),
+                                  scales=vscales[key][:, w * b:w * b + w],
+                                  in_=vgrp[(key, b)][:].rearrange("p g d j -> p (g d j)"))
+
+        def quantise(src, tagc, tags):
+            codes = wk.tile([P, N], U32, name=tagc, tag=tagc, align_bytes=64)
+            scales = wk.tile([P, N], U8, name=tags, tag=tags, align_bytes=64)
+            nc.vector.quantize_mx(
+                out=codes[:].bitcast(FP8X4),
+                scales=scales[:],
+                in_=src[:].rearrange("p n t -> p (n t)"),
+            )
+            return codes, scales
+
+        def ok(g):
+            return 0 <= g < NH
+
+        def load(g):
+            s = {}
+            st[g] = s
+            s["nr"] = ld.tile([P, 4, N], BF16, name="nr", tag="nr")
+            nc.sync.dma_start(out=s["nr"][:], in_=wr_v[g])
+            s["nd"] = ld.tile([P, 4, N], BF16, name="nd", tag="nd")
+            nc.sync.dma_start(out=s["nd"][:], in_=wd_v[g])
+
+        def x4(g):
+            s = st[g]
+            s["x4r"] = wk.tile([P, 4, N], F32, name="x4r", tag="x4r", bufs=3)
+            s["x4d"] = wk.tile([P, 4, N], F32, name="x4d", tag="x4d", bufs=3)
+            s["rs"] = wk.tile([P, 8], F32, name="rs", tag="rs")
+            for m, (dst, src) in enumerate(((s["x4r"], s["nr"]), (s["x4d"], s["nd"]))):
+                for t in range(4):
+                    nc.scalar.activation(out=dst[:, t, :], in_=src[:, t, :], func=ACT.Copy, scale=BETA,
+                                         accum_out=s["rs"][:, 4 * m + t:4 * m + t + 1])
+
+        def rsq(g):
+            s = st[g]
+            inv = wk.tile([P, 8], F32, name="inv", tag="inv")
+            nc.vector.reciprocal(out=inv[:], in_=s["rs"][:])
+            s["dr"] = wk.tile([P, 8], F32, name="dr", tag="dr")
+            nc.scalar.activation(out=s["dr"][:], in_=inv[:], func=ACT.Sqrt, scale=BETA)
+
+        def dbc(g, m):
+            s = st[g]
+            db = ps.tile([P, N], F32, name="dbc", tag="dbc", bufs=2)
+            for c in range(4):
+                nc.tensor.transpose(db[:, P * c:P * c + P],
+                                    s["dr"][:, 4 * m + c:4 * m + c + 1].to_broadcast([P, P]), ident[:])
+            s["dbc%d" % m] = db
+
+        def wkmul(g, m):
+            s = st[g]
+            src = s["nr"] if m == 0 else s["nd"]
+            w = wk.tile([P, 4, N], F32, name="wk%d" % m, tag="wk%d" % m)
+            for t in range(4):
+                nc.gpsimd.tensor_scalar(out=w[:, t, :], in0=src[:, t, :],
+                                        scalar1=s["dr"][:, 4 * m + t:4 * m + t + 1], scalar2=0.0,
+                                        op0=ALU.mult, op1=ALU.add)
+            s["wk%d" % m] = w
+
+        def wdt(g, b2):
+            s = st[g]
+            if b2 == 0:
+                s["gd"] = wk.tile([P, N, 4], BF16, name="gd", tag="gd", align_bytes=64)
+            nd32 = s["nd"][:].bitcast(F32)
+            wt = ps.tile([P, 2, 256], F32, name="wt", tag="misc", bufs=2)
+            for ii in range(2):
+                for u in range(2):
+                    nc.tensor.transpose(wt[:, u, P * ii:P * ii + P],
+                                        nd32[:, 2 * b2 + ii, P * u:P * u + P], ident[:])
+            s["wt%d" % b2] = wt
+
+        def wdtc(g, b2):
+            s = st[g]
+            gd32 = s["gd"][:].bitcast(F32)
+            nc.scalar.copy(out=gd32[:, 256 * b2:256 * b2 + 256, :],
+                           in_=s["wt%d" % b2][:].rearrange("p u n -> p n u"))
+
+        def tt(g, m):
+            s = st[g]
+            gs = wk.tile([P, N, 4], BF16, name="gs%d" % m, tag="gs%d" % m, align_bytes=64)
+            nc.vector.tensor_tensor(out=gs[:], in0=s["wk%d" % m][:].rearrange("p t n -> p n t"),
+                                    in1=s["dbc%d" % m][:].unsqueeze(2).to_broadcast([P, N, 4]), op=ALU.mult)
+            s["gs%d" % m] = gs
+
+        def q_s(g, m):
+            st[g]["cs%d" % m] = quantise(st[g]["gs%d" % m], "c%d" % m, "s%d" % m)
+
+        def q_w(g):
+            st[g]["cw"] = quantise(st[g]["gd"], "cw", "sw")
+
+        def p_pass(g, i):
+            s = st[g]
+            cr, sr = s["cs0"]
+            cd, sd = s["cs1"]
+            pp = ps.tile([P, N], F32, name="pp", tag="pp", bufs=2)
+            nc.tensor.matmul_mx(out=pp[:], lhsT=cr[:, P * i:P * i + P].bitcast(FP8X4),
+                                lhsT_scale=sr[:, P * i:P * i + P],
+                                rhs=cd[:].bitcast(FP8X4), rhs_scale=sd[:], start=True, stop=True)
+            s["pp%d" % i] = pp
+
+        def e3(g, i):
+            s = st[g]
+            nc.vector.scalar_tensor_tensor(out=s["x4r"][:, i, :], in0=s["pp%d" % i][:], scalar=ALPHA,
+                                           in1=s["x4r"][:, i, :], op0=ALU.mult, op1=ALU.add)
+
+        def at(g, i):
+            s = st[g]
+            a = ps.tile([P, 4, P], F32, name="at", tag="at", bufs=2)
+            for j in range(4):
+                nc.tensor.matmul(out=a[:, j, :], lhsT=s["x4r"][:, i, P * j:P * j + P], rhs=ident[:],
+                                 is_transpose=True, start=True, stop=False)
+                nc.tensor.matmul(out=a[:, j, :], lhsT=s["x4d"][:, i, P * j:P * j + P], rhs=ident[:],
+                                 is_transpose=True, start=False, stop=True)
+            s["at%d" % i] = a
+
+        def at_copy(g, i):
+            s = st[g]
+            if i == 0:
+                s["ga"] = wk.tile([P, N, 4], BF16, name="ga", tag="ga", align_bytes=64)
+            nc.scalar.copy(out=s["ga"][:, P * i:P * i + P, :], in_=s["at%d" % i][:].rearrange("p j n -> p n j"))
+
+        def q_a(g):
+            st[g]["ca"] = quantise(st[g]["ga"], "ca", "sa")
+
+        def av(g):
+            s = st[g]
+            ob = ps.tile([P, 2, 4, HD], F32, name="ob", tag="misc", bufs=2)
+            for o, key in enumerate(("t", "w")):
+                cc, ss = s["ca"] if o == 0 else s["cw"]
+                for i in range(4):
+                    nc.tensor.matmul_mx(out=ob[:, o, i, :], lhsT=cc[:, P * i:P * i + P].bitcast(FP8X4),
+                                        lhsT_scale=ss[:, P * i:P * i + P],
+                                        rhs=vcodes[key][:, HD * g:HD * g + HD].bitcast(FP8X4),
+                                        rhs_scale=vscales[key][:, HD * g:HD * g + HD],
+                                        start=True, stop=True)
+            s["ob"] = ob
+
+        def ocopy(g):
+            b = g // NHB
+            h = g % NHB
+            if h == 0:
+                st["o"] = const.tile([P, 2, 4, N], F32, name="obig", tag="obig")
+            obig = st["o"]
+            nc.scalar.copy(out=obig[:, :, :, HD * h:HD * h + HD], in_=st[g]["ob"][:])
+            last = g >= NH - 2
+            if last or h % 2 == 1:
+                c0 = HD * h if last else HD * (h - 1)
+                c1 = HD * (h + 1)
+                for o, dst in enumerate((out_rd, out_d)):
+                    nc.sync.dma_start(out=dst[b].rearrange("(i p) c -> p i c", p=P)[:, :, c0:c1],
+                                      in_=obig[:, o, :, c0:c1])
+
+        STEPS = (
+            ("load", 3), ("tt", 0, 0), ("dbc", 1, 0), ("tt", 0, 1), ("dbc", 1, 1),
+            ("q_s", 0, 0), ("q_s", 0, 1), ("p_pass", 0, 0), ("p_pass", 0, 1), ("q_a", -1), ("av", -1),
+            ("e3", 0, 0), ("p_pass", 0, 2), ("e3", 0, 1), ("p_pass", 0, 3),
+            ("x4", 2), ("ocopy", -1), ("rsq", 2), ("wkmul", 2, 0), ("wkmul", 2, 1),
+            ("e3", 0, 2), ("e3", 0, 3), ("q_w", 0),
+            ("at", 0, 0), ("at", 0, 1), ("wdt", 1, 0), ("at_copy", 0, 0), ("at", 0, 2), ("at_copy", 0, 1),
+            ("wdtc", 1, 0), ("at", 0, 3), ("wdt", 1, 1), ("at_copy", 0, 2), ("at_copy", 0, 3), ("wdtc", 1, 1),
+        )
+        FN = {"load": load, "tt": tt, "dbc": dbc, "q_s": q_s, "p_pass": p_pass, "q_a": q_a, "av": av, "e3": e3,
+              "x4": x4, "ocopy": ocopy, "rsq": rsq, "wkmul": wkmul, "q_w": q_w, "at": at, "wdt": wdt,
+              "at_copy": at_copy, "wdtc": wdtc}
+        EXTRA = {(-2, "wkmul"): (vreg, "t", 0), (-1, "wkmul"): (vreg, "w", 0), (0, "q_w"): (q_v, "t", 0),
+                 (1, "q_s"): (q_v, "w", 0), (3, "wkmul"): (vreg, "t", 1), (4, "wkmul"): (vreg, "w", 1),
+                 (5, "q_w"): (q_v, "t", 1), (6, "q_w"): (q_v, "w", 1)}
+        load(0)
+        load(1)
+        vload("t")
+        load(2)
+        vload("w")
+        for it in range(-2, NH + 1):
+            for step in STEPS:
+                g = it + step[1]
+                if not ok(g) or (step[0] == "load" and g < 3):
+                    continue
+                FN[step[0]](g, *step[2:])
+                if step[-1] != 0 or len(step) == 2:
+                    ex = EXTRA.get((it, step[0]))
+                    if ex:
+                        ex[0](*ex[1:])

@@ -112,8 +112,11 @@ def tile_multiattention_pa_kernel(tc, attn_r, attn_d, v_d, out_rd, out_d):
             s = st[g]
             db = ps.tile([P, N], F32, name="dbc", tag="dbc", bufs=2)
             for c in range(4):
-                nc.tensor.transpose(db[:, P * c:P * c + P],
-                                    s["dr"][:, 4 * m + c:4 * m + c + 1].to_broadcast([P, P]), ident[:])
+                col = s["dr"][:, 4 * m + c:4 * m + c + 1].to_broadcast([P, P])
+                if m == 1 and c == 3:
+                    nc.tensor.transpose(db[:, P * c:P * c + P], col, ident[:])
+                else:
+                    nc.tensor.matmul(out=db[:, P * c:P * c + P], lhsT=col, rhs=ident[:], start=True, stop=True)
             s["dbc%d" % m] = db
 
         def wkmul(g, m):

@@ -24,6 +24,21 @@ BETA = 0.4
 
 FLOPS = NH * (2 * N * N * N + 2 * 2 * N * N * HD)
 
+PLAIN = (
+    ("dbc", 1, 0), ("dbc", 0, 3), ("at", 1, 2), ("dbc", 1, 3),
+    ("at", 2, 2), ("dbc", 0, 2), ("dbc", 0, 0),
+)
+STEPS = (
+    ("dbc", 1, 0), ("load", 3), ("q_s", 0, 1), ("q_a", -1), ("dbc", 1, 1),
+    ("p_pass", 0, 0), ("q_w", 0), ("p_pass", 0, 1), ("av", -1), ("e3", 0, 0),
+    ("p_pass", 0, 2), ("e3", 0, 1), ("e3", 0, 2), ("p_pass", 0, 3), ("e3", 0, 3),
+    ("at", 0, 0), ("at", 0, 1), ("ocopy", -1), ("recip", 2), ("wdt", 1, 0),
+    ("at_copy", 0, 0), ("sq", 2), ("at_copy", 0, 1), ("wkmul", 2, 0), ("wdt", 1, 1),
+    ("wkmul", 2, 1), ("tt", 1, 0), ("tt", 1, 1), ("wdtc", 1, 0), ("wdtc", 1, 1),
+    ("at", 0, 2), ("at_copy", 0, 2), ("at", 0, 3), ("at_copy", 0, 3), ("x4", 3),
+    ("q_s", 1, 0),
+)
+
 
 def tile_multiattention_pa_kernel(tc, attn_r, attn_d, v_d, out_rd, out_d):
     nc = tc.nc
@@ -101,10 +116,14 @@ def tile_multiattention_pa_kernel(tc, attn_r, attn_d, v_d, out_rd, out_d):
                     nc.scalar.activation(out=dst[:, t, :], in_=src[:, t, :], func=ACT.Copy, scale=BETA,
                                          accum_out=s["rs"][:, 4 * m + t:4 * m + t + 1])
 
-        def rsq(g):
+        def recip(g):
             s = st[g]
-            inv = wk.tile([P, 8], F32, name="inv", tag="inv")
-            nc.vector.reciprocal(out=inv[:], in_=s["rs"][:])
+            s["inv"] = wk.tile([P, 8], F32, name="inv", tag="inv")
+            nc.vector.reciprocal(out=s["inv"][:], in_=s["rs"][:])
+
+        def sq(g):
+            s = st[g]
+            inv = s["inv"]
             s["dr"] = wk.tile([P, 8], F32, name="dr", tag="dr")
             nc.scalar.activation(out=s["dr"][:], in_=inv[:], func=ACT.Sqrt, scale=BETA)
 
@@ -113,10 +132,10 @@ def tile_multiattention_pa_kernel(tc, attn_r, attn_d, v_d, out_rd, out_d):
             db = ps.tile([P, N], F32, name="dbc", tag="dbc", bufs=2)
             for c in range(4):
                 col = s["dr"][:, 4 * m + c:4 * m + c + 1].to_broadcast([P, P])
-                if m == 1 and c == 3:
-                    nc.tensor.transpose(db[:, P * c:P * c + P], col, ident[:])
-                else:
+                if ("dbc", m, c) in PLAIN:
                     nc.tensor.matmul(out=db[:, P * c:P * c + P], lhsT=col, rhs=ident[:], start=True, stop=True)
+                else:
+                    nc.tensor.transpose(db[:, P * c:P * c + P], col, ident[:])
             s["dbc%d" % m] = db
 
         def wkmul(g, m):
@@ -182,7 +201,7 @@ def tile_multiattention_pa_kernel(tc, attn_r, attn_d, v_d, out_rd, out_d):
                 nc.tensor.matmul(out=a[:, j, :], lhsT=s["x4r"][:, i, P * j:P * j + P], rhs=ident[:],
                                  is_transpose=True, start=True, stop=False)
                 nc.tensor.matmul(out=a[:, j, :], lhsT=s["x4d"][:, i, P * j:P * j + P], rhs=ident[:],
-                                 is_transpose=True, start=False, stop=True)
+                                 is_transpose=(("at", i, j) not in PLAIN), start=False, stop=True)
             s["at%d" % i] = a
 
         def at_copy(g, i):
@@ -222,17 +241,8 @@ def tile_multiattention_pa_kernel(tc, attn_r, attn_d, v_d, out_rd, out_d):
                     nc.sync.dma_start(out=dst[b].rearrange("(i p) c -> p i c", p=P)[:, :, c0:c1],
                                       in_=obig[:, o, :, c0:c1])
 
-        STEPS = (
-            ("load", 3), ("tt", 0, 0), ("dbc", 1, 0), ("tt", 0, 1), ("dbc", 1, 1),
-            ("q_s", 0, 0), ("q_s", 0, 1), ("p_pass", 0, 0), ("p_pass", 0, 1), ("q_a", -1), ("av", -1),
-            ("e3", 0, 0), ("p_pass", 0, 2), ("e3", 0, 1), ("p_pass", 0, 3),
-            ("x4", 2), ("ocopy", -1), ("rsq", 2), ("wkmul", 2, 0), ("wkmul", 2, 1),
-            ("e3", 0, 2), ("e3", 0, 3), ("q_w", 0),
-            ("at", 0, 0), ("at", 0, 1), ("wdt", 1, 0), ("at_copy", 0, 0), ("at", 0, 2), ("at_copy", 0, 1),
-            ("wdtc", 1, 0), ("at", 0, 3), ("wdt", 1, 1), ("at_copy", 0, 2), ("at_copy", 0, 3), ("wdtc", 1, 1),
-        )
         FN = {"load": load, "tt": tt, "dbc": dbc, "q_s": q_s, "p_pass": p_pass, "q_a": q_a, "av": av, "e3": e3,
-              "x4": x4, "ocopy": ocopy, "rsq": rsq, "wkmul": wkmul, "q_w": q_w, "at": at, "wdt": wdt,
+              "x4": x4, "ocopy": ocopy, "recip": recip, "sq": sq, "wkmul": wkmul, "q_w": q_w, "at": at, "wdt": wdt,
               "at_copy": at_copy, "wdtc": wdtc}
         EXTRA = {(-2, "wkmul"): (vreg, "t", 0), (-1, "wkmul"): (vreg, "w", 0), (0, "q_w"): (q_v, "t", 0),
                  (1, "q_s"): (q_v, "w", 0), (3, "wkmul"): (vreg, "t", 1), (4, "wkmul"): (vreg, "w", 1),
@@ -242,7 +252,7 @@ def tile_multiattention_pa_kernel(tc, attn_r, attn_d, v_d, out_rd, out_d):
         vload("t")
         load(2)
         vload("w")
-        for it in range(-2, NH + 1):
+        for it in range(-4, NH + 3):
             for step in STEPS:
                 g = it + step[1]
                 if not ok(g) or (step[0] == "load" and g < 3):

@@ -25,18 +25,17 @@ BETA = 0.4
 FLOPS = NH * (2 * N * N * N + 2 * 2 * N * N * HD)
 
 PLAIN = (
-    ("dbc", 1, 0), ("dbc", 0, 3), ("at", 1, 2), ("dbc", 1, 3),
-    ("at", 2, 2), ("dbc", 0, 2), ("dbc", 0, 0),
+    ("dbc", 1, 0), ("at", 1, 1), ("at", 2, 1), ("at", 1, 3),
+    ("dbc", 0, 1), ("at", 3, 2), ("dbc", 1, 1),
 )
 STEPS = (
-    ("dbc", 1, 0), ("load", 3), ("q_s", 0, 1), ("q_a", -1), ("dbc", 1, 1),
-    ("p_pass", 0, 0), ("q_w", 0), ("p_pass", 0, 1), ("av", -1), ("e3", 0, 0),
-    ("p_pass", 0, 2), ("e3", 0, 1), ("e3", 0, 2), ("p_pass", 0, 3), ("e3", 0, 3),
-    ("at", 0, 0), ("at", 0, 1), ("ocopy", -1), ("recip", 2), ("wdt", 1, 0),
-    ("at_copy", 0, 0), ("sq", 2), ("at_copy", 0, 1), ("wkmul", 2, 0), ("wdt", 1, 1),
-    ("wkmul", 2, 1), ("tt", 1, 0), ("tt", 1, 1), ("wdtc", 1, 0), ("wdtc", 1, 1),
-    ("at", 0, 2), ("at_copy", 0, 2), ("at", 0, 3), ("at_copy", 0, 3), ("x4", 3),
-    ("q_s", 1, 0),
+    ("wdtc", 0, 1), ("load", 3), ("at_copy", -1, 2), ("q_s", 0), ("at_copy", -1, 3),
+    ("q_a", -1), ("dbc", 1, 0), ("dbc", 1, 1), ("p_pass", 0, 0), ("p_pass", 0, 1),
+    ("av", -1), ("e3", 0, 0), ("e3", 0, 1), ("gate", 2), ("x4", 2),
+    ("p_pass", 0, 2), ("p_pass", 0, 3), ("wdtc", 0, 0), ("at", 0, 0), ("recip", 2),
+    ("at", 0, 1), ("e3", 0, 2), ("wkmul", 1, 1), ("wdt", 1, 1), ("sq", 2),
+    ("at_copy", 0, 0), ("at_copy", 0, 1), ("e3", 0, 3), ("at", 0, 2), ("ocopy", -1),
+    ("at", 0, 3), ("wkmul", 2, 0), ("tt", 1, 0), ("wdt", 1, 0), ("tt", 1, 1),
 )
 
 
@@ -75,8 +74,11 @@ def tile_multiattention_pa_kernel(tc, attn_r, attn_d, v_d, out_rd, out_d):
 
         def vreg(key, b):
             grp = const.tile([P, NHB, HD, 4], BF16, name="vgrp", tag="vgrp", bufs=2, align_bytes=64)
-            nc.gpsimd.tensor_scalar(out=grp[:], in0=vraw[key][:, NHB * b:NHB * b + NHB].rearrange("p g j d -> p g d j"),
-                                    scalar1=1.0, scalar2=0.0, op0=ALU.mult, op1=ALU.add)
+            src = vraw[key][:, NHB * b:NHB * b + NHB].rearrange("p g j d -> p g d j")
+            if b == 0:
+                nc.vector.tensor_copy(out=grp[:], in_=src)
+            else:
+                nc.gpsimd.tensor_scalar(out=grp[:], in0=src, scalar1=1.0, scalar2=0.0, op0=ALU.mult, op1=ALU.add)
             vgrp[(key, b)] = grp
 
         def q_v(key, b):
@@ -86,12 +88,12 @@ def tile_multiattention_pa_kernel(tc, attn_r, attn_d, v_d, out_rd, out_d):
                                   in_=vgrp[(key, b)][:].rearrange("p g d j -> p (g d j)"))
 
         def quantise(src, tagc, tags):
-            codes = wk.tile([P, N], U32, name=tagc, tag=tagc, align_bytes=64)
-            scales = wk.tile([P, N], U8, name=tags, tag=tags, align_bytes=64)
+            codes = wk.tile([P, 2, N], U32, name=tagc, tag=tagc, align_bytes=64)
+            scales = wk.tile([P, 2, N], U8, name=tags, tag=tags, align_bytes=64)
             nc.vector.quantize_mx(
-                out=codes[:].bitcast(FP8X4),
-                scales=scales[:],
-                in_=src[:].rearrange("p n t -> p (n t)"),
+                out=codes[:].rearrange("p a n -> p (a n)").bitcast(FP8X4),
+                scales=scales[:].rearrange("p a n -> p (a n)"),
+                in_=src[:].rearrange("p a n t -> p (a n t)"),
             )
             return codes, scales
 
@@ -127,6 +129,10 @@ def tile_multiattention_pa_kernel(tc, attn_r, attn_d, v_d, out_rd, out_d):
             s["dr"] = wk.tile([P, 8], F32, name="dr", tag="dr")
             nc.scalar.activation(out=s["dr"][:], in_=inv[:], func=ACT.Sqrt, scale=BETA)
 
+        def gate(g):
+            st[g]["zero"] = wk.tile([P, 8], F32, name="zero", tag="zero")
+            nc.vector.memset(st[g]["zero"][:], 0.0)
+
         def dbc(g, m):
             s = st[g]
             db = ps.tile([P, N], F32, name="dbc", tag="dbc", bufs=2)
@@ -144,14 +150,14 @@ def tile_multiattention_pa_kernel(tc, attn_r, attn_d, v_d, out_rd, out_d):
             w = wk.tile([P, 4, N], F32, name="wk%d" % m, tag="wk%d" % m)
             for t in range(4):
                 nc.gpsimd.tensor_scalar(out=w[:, t, :], in0=src[:, t, :],
-                                        scalar1=s["dr"][:, 4 * m + t:4 * m + t + 1], scalar2=0.0,
+                                        scalar1=s["dr"][:, 4 * m + t:4 * m + t + 1], scalar2=s["zero"][:, 0:1],
                                         op0=ALU.mult, op1=ALU.add)
             s["wk%d" % m] = w
 
         def wdt(g, b2):
             s = st[g]
             if b2 == 0:
-                s["gd"] = wk.tile([P, N, 4], BF16, name="gd", tag="gd", align_bytes=64)
+                s["gaw"] = wk.tile([P, 2, N, 4], BF16, name="gaw", tag="gaw", bufs=3, align_bytes=64)
             nd32 = s["nd"][:].bitcast(F32)
             wt = ps.tile([P, 2, 256], F32, name="wt", tag="misc", bufs=2)
             for ii in range(2):
@@ -162,31 +168,31 @@ def tile_multiattention_pa_kernel(tc, attn_r, attn_d, v_d, out_rd, out_d):
 
         def wdtc(g, b2):
             s = st[g]
-            gd32 = s["gd"][:].bitcast(F32)
+            gd32 = s["gaw"][:, 1].bitcast(F32)
             nc.scalar.copy(out=gd32[:, 256 * b2:256 * b2 + 256, :],
                            in_=s["wt%d" % b2][:].rearrange("p u n -> p n u"))
 
         def tt(g, m):
             s = st[g]
-            gs = wk.tile([P, N, 4], BF16, name="gs%d" % m, tag="gs%d" % m, align_bytes=64)
-            nc.vector.tensor_tensor(out=gs[:], in0=s["wk%d" % m][:].rearrange("p t n -> p n t"),
-                                    in1=s["dbc%d" % m][:].unsqueeze(2).to_broadcast([P, N, 4]), op=ALU.mult)
-            s["gs%d" % m] = gs
+            if m == 0:
+                s["gs"] = wk.tile([P, 2, N, 4], BF16, name="gs", tag="gs", align_bytes=64)
+            gs = s["gs"]
+            nc.vector.tensor_tensor(
+                out=gs[:, m].rearrange("p (c i) t -> p c t i", i=4),
+                in0=s["wk%d" % m][:].rearrange("p t (c i) -> p c t i", i=4),
+                in1=s["dbc%d" % m][:].rearrange("p (c i) -> p c i", i=4).unsqueeze(2).to_broadcast([P, N // 4, 4, 4]),
+                op=ALU.mult)
 
-        def q_s(g, m):
-            st[g]["cs%d" % m] = quantise(st[g]["gs%d" % m], "c%d" % m, "s%d" % m)
-
-        def q_w(g):
-            st[g]["cw"] = quantise(st[g]["gd"], "cw", "sw")
+        def q_s(g):
+            st[g]["cs"] = quantise(st[g]["gs"], "cs", "ss")
 
         def p_pass(g, i):
             s = st[g]
-            cr, sr = s["cs0"]
-            cd, sd = s["cs1"]
+            cs, ss = s["cs"]
             pp = ps.tile([P, N], F32, name="pp", tag="pp", bufs=2)
-            nc.tensor.matmul_mx(out=pp[:], lhsT=cr[:, P * i:P * i + P].bitcast(FP8X4),
-                                lhsT_scale=sr[:, P * i:P * i + P],
-                                rhs=cd[:].bitcast(FP8X4), rhs_scale=sd[:], start=True, stop=True)
+            nc.tensor.matmul_mx(out=pp[:], lhsT=cs[:, 0, P * i:P * i + P].bitcast(FP8X4),
+                                lhsT_scale=ss[:, 0, P * i:P * i + P],
+                                rhs=cs[:, 1, :].bitcast(FP8X4), rhs_scale=ss[:, 1, :], start=True, stop=True)
             s["pp%d" % i] = pp
 
         def e3(g, i):
@@ -206,21 +212,19 @@ def tile_multiattention_pa_kernel(tc, attn_r, attn_d, v_d, out_rd, out_d):
 
         def at_copy(g, i):
             s = st[g]
-            if i == 0:
-                s["ga"] = wk.tile([P, N, 4], BF16, name="ga", tag="ga", align_bytes=64)
-            nc.scalar.copy(out=s["ga"][:, P * i:P * i + P, :], in_=s["at%d" % i][:].rearrange("p j n -> p n j"))
+            nc.scalar.copy(out=s["gaw"][:, 0, P * i:P * i + P, :], in_=s["at%d" % i][:].rearrange("p j n -> p n j"))
 
         def q_a(g):
-            st[g]["ca"] = quantise(st[g]["ga"], "ca", "sa")
+            st[g]["ca"] = quantise(st[g]["gaw"], "ca", "sa")
 
         def av(g):
             s = st[g]
             ob = ps.tile([P, 2, 4, HD], F32, name="ob", tag="misc", bufs=2)
             for o, key in enumerate(("t", "w")):
-                cc, ss = s["ca"] if o == 0 else s["cw"]
+                cc, ss = s["ca"]
                 for i in range(4):
-                    nc.tensor.matmul_mx(out=ob[:, o, i, :], lhsT=cc[:, P * i:P * i + P].bitcast(FP8X4),
-                                        lhsT_scale=ss[:, P * i:P * i + P],
+                    nc.tensor.matmul_mx(out=ob[:, o, i, :], lhsT=cc[:, o, P * i:P * i + P].bitcast(FP8X4),
+                                        lhsT_scale=ss[:, o, P * i:P * i + P],
                                         rhs=vcodes[key][:, HD * g:HD * g + HD].bitcast(FP8X4),
                                         rhs_scale=vscales[key][:, HD * g:HD * g + HD],
                                         start=True, stop=True)
@@ -242,16 +246,18 @@ def tile_multiattention_pa_kernel(tc, attn_r, attn_d, v_d, out_rd, out_d):
                                       in_=obig[:, o, :, c0:c1])
 
         FN = {"load": load, "tt": tt, "dbc": dbc, "q_s": q_s, "p_pass": p_pass, "q_a": q_a, "av": av, "e3": e3,
-              "x4": x4, "ocopy": ocopy, "recip": recip, "sq": sq, "wkmul": wkmul, "q_w": q_w, "at": at, "wdt": wdt,
-              "at_copy": at_copy, "wdtc": wdtc}
-        EXTRA = {(-2, "wkmul"): (vreg, "t", 0), (-1, "wkmul"): (vreg, "w", 0), (0, "q_w"): (q_v, "t", 0),
-                 (1, "q_s"): (q_v, "w", 0), (3, "wkmul"): (vreg, "t", 1), (4, "wkmul"): (vreg, "w", 1),
-                 (5, "q_w"): (q_v, "t", 1), (6, "q_w"): (q_v, "w", 1)}
+              "x4": x4, "ocopy": ocopy, "recip": recip, "sq": sq, "wkmul": wkmul, "at": at, "wdt": wdt,
+              "at_copy": at_copy, "wdtc": wdtc, "gate": gate}
+        EXTRA = {(3, "wkmul"): (vreg, "t", 1), (4, "wkmul"): (vreg, "w", 1),
+                 (5, "q_s"): (q_v, "t", 1), (6, "q_s"): (q_v, "w", 1)}
         load(0)
         load(1)
         vload("t")
         load(2)
         vload("w")
+        for key in ("t", "w"):
+            vreg(key, 0)
+            q_v(key, 0)
         for it in range(-4, NH + 3):
             for step in STEPS:
                 g = it + step[1]

@@ -24,18 +24,51 @@ BETA = 0.4
 
 FLOPS = NH * (2 * N * N * N + 2 * 2 * N * N * HD)
 
+ENG = {"wk0": "g", "wk1": "s", "wk2": "g", "wk3": "g", "wk4": "g", "wk5": "g", "wk6": "s", "wk7": "g", "at0": "s", "at1": "s", "at2": "s", "at3": "s", "wd0": "s", "wd1": "s", "oc": "s", "x0": "s", "x1": "s", "x2": "s", "x3": "s", "x4": "s", "x5": "s", "x6": "s", "x7": "s"}
+ENG_PRO = {"wk0": "s", "wk1": "v", "wk2": "g", "wk3": "s", "wk4": "s", "wk5": "s", "wk6": "v", "wk7": "s", "at0": "s", "at1": "s", "at2": "s", "at3": "s", "wd0": "s", "wd1": "s", "oc": "s", "x0": "v", "x1": "s", "x2": "v", "x3": "s", "x4": "v", "x5": "v", "x6": "s", "x7": "s"}
+ENG_EPI = {"wk0": "g", "wk1": "g", "wk2": "s", "wk3": "g", "wk4": "s", "wk5": "g", "wk6": "g", "wk7": "s", "at0": "s", "at1": "v", "at2": "v", "at3": "s", "wd0": "s", "wd1": "s", "oc": "s", "x0": "s", "x1": "s", "x2": "s", "x3": "s", "x4": "s", "x5": "s", "x6": "s", "x7": "s"}
 PLAIN = (
-    ("dbc", 1, 0), ("at", 1, 1), ("at", 2, 1), ("at", 1, 3),
-    ("dbc", 0, 1), ("at", 3, 2), ("dbc", 1, 1),
+    ("dbc", 1, 0), ("dbc", 0, 1), ("at", 2, 3), ("at", 3, 3), ("at", 0, 2),
+    ("at", 3, 2), ("at", 2, 1),
 )
 STEPS = (
-    ("wdtc", 0, 1), ("load", 3), ("at_copy", -1, 2), ("q_s", 0), ("at_copy", -1, 3),
-    ("q_a", -1), ("dbc", 1, 0), ("dbc", 1, 1), ("p_pass", 0, 0), ("p_pass", 0, 1),
-    ("av", -1), ("e3", 0, 0), ("e3", 0, 1), ("gate", 2), ("x4", 2),
-    ("p_pass", 0, 2), ("p_pass", 0, 3), ("wdtc", 0, 0), ("at", 0, 0), ("recip", 2),
-    ("at", 0, 1), ("e3", 0, 2), ("wkmul", 1, 1), ("wdt", 1, 1), ("sq", 2),
-    ("at_copy", 0, 0), ("at_copy", 0, 1), ("e3", 0, 3), ("at", 0, 2), ("ocopy", -1),
-    ("at", 0, 3), ("wkmul", 2, 0), ("tt", 1, 0), ("wdt", 1, 0), ("tt", 1, 1),
+    ("q_s", 0), ("vreg", 1, "t"), ("q_v", 1, "t"), ("p_pass", 0, 0), ("q_a", -1),
+    ("p_pass", 0, 1), ("gate", 2), ("p_pass", 0, 2), ("av", -1), ("wkmul", 2, 1, 0),
+    ("e3", 0, 0), ("load", 4), ("wkmul", 2, 1, 3), ("p_pass", 0, 3), ("dbc", 1, 0),
+    ("at", 0, 0), ("e3", 0, 1), ("vreg", 1, "w"), ("e3", 0, 2), ("e3", 0, 3),
+    ("at", 0, 1), ("at_copy", 0, 0), ("ocopy", -1), ("dbc", 1, 1), ("at_copy", 0, 1),
+    ("wkmul", 2, 0, 0), ("wkmul", 2, 1, 1), ("wdt", 1, 0), ("tt", 1, 0), ("at", 0, 3),
+    ("recip", 3), ("wkmul", 2, 1, 2), ("at", 0, 2), ("wkmul", 2, 0, 1), ("tt", 1, 1),
+    ("at_copy", 0, 3), ("x4", 4, 0, 0), ("wdt", 1, 1), ("q_v", 1, "w"), ("at_copy", 0, 2),
+    ("wkmul", 2, 0, 2), ("x4", 4, 1, 0), ("sq", 3), ("wdtc", 1, 0), ("x4", 4, 1, 1),
+    ("x4", 4, 1, 2), ("x4", 4, 0, 1), ("wdtc", 1, 1), ("x4", 4, 0, 2), ("x4", 4, 1, 3),
+    ("wkmul", 2, 0, 3), ("x4", 4, 0, 3),
+)
+STEPS_PRO = (
+    ("q_s", 0), ("p_pass", 0, 0), ("e3", 0, 0), ("gate", 2), ("p_pass", 0, 1),
+    ("wkmul", 2, 0, 0), ("wkmul", 2, 0, 3), ("p_pass", 0, 3), ("dbc", 1, 0), ("e3", 0, 3),
+    ("wkmul", 2, 1, 0), ("e3", 0, 1), ("vreg", 1, "t"), ("p_pass", 0, 2), ("tt", 1, 0),
+    ("q_a", -1), ("at", 0, 0), ("wkmul", 2, 1, 3), ("wkmul", 2, 0, 2), ("e3", 0, 2),
+    ("at", 0, 1), ("ocopy", -1), ("dbc", 1, 1), ("wdt", 1, 1), ("at_copy", 0, 0),
+    ("q_v", 1, "t"), ("tt", 1, 1), ("wkmul", 2, 0, 1), ("at", 0, 3), ("vreg", 1, "w"),
+    ("load", 4), ("at_copy", 0, 1), ("recip", 3), ("at_copy", 0, 3), ("av", -1),
+    ("wkmul", 2, 1, 2), ("at", 0, 2), ("wdt", 1, 0), ("at_copy", 0, 2), ("wdtc", 1, 1),
+    ("x4", 4, 0, 0), ("x4", 4, 0, 1), ("wkmul", 2, 1, 1), ("x4", 4, 0, 2), ("x4", 4, 1, 1),
+    ("x4", 4, 0, 3), ("x4", 4, 1, 3), ("sq", 3), ("x4", 4, 1, 2), ("x4", 4, 1, 0),
+    ("wdtc", 1, 0), ("q_v", 1, "w"),
+)
+STEPS_EPI = (
+    ("wkmul", 2, 0, 3), ("q_s", 0), ("p_pass", 0, 0), ("q_a", -1), ("load", 4),
+    ("p_pass", 0, 1), ("wkmul", 2, 0, 2), ("wdt", 1, 0), ("e3", 0, 0), ("e3", 0, 1),
+    ("x4", 4, 0, 1), ("p_pass", 0, 3), ("q_v", 1, "t"), ("wkmul", 2, 0, 1), ("wdtc", 1, 0),
+    ("wkmul", 2, 1, 0), ("p_pass", 0, 2), ("q_v", 1, "w"), ("e3", 0, 3), ("x4", 4, 1, 0),
+    ("dbc", 1, 0), ("wkmul", 2, 1, 2), ("vreg", 1, "w"), ("at", 0, 0), ("wdt", 1, 1),
+    ("wkmul", 2, 0, 0), ("dbc", 1, 1), ("x4", 4, 1, 3), ("e3", 0, 2), ("at", 0, 1),
+    ("tt", 1, 0), ("tt", 1, 1), ("x4", 4, 0, 3), ("x4", 4, 0, 0), ("at_copy", 0, 0),
+    ("x4", 4, 1, 1), ("at", 0, 3), ("at_copy", 0, 1), ("wkmul", 2, 1, 3), ("at_copy", 0, 3),
+    ("at", 0, 2), ("av", -1), ("sq", 3), ("wdtc", 1, 1), ("at_copy", 0, 2),
+    ("vreg", 1, "t"), ("ocopy", -1), ("recip", 3), ("x4", 4, 0, 2), ("gate", 2),
+    ("x4", 4, 1, 2), ("wkmul", 2, 1, 1),
 )
 
 
@@ -73,7 +106,7 @@ def tile_multiattention_pa_kernel(tc, attn_r, attn_d, v_d, out_rd, out_d):
             vscales[key] = const.tile([P, NH * HD], U8, name="vs_" + key, align_bytes=64)
 
         def vreg(key, b):
-            grp = const.tile([P, NHB, HD, 4], BF16, name="vgrp", tag="vgrp", bufs=2, align_bytes=64)
+            grp = const.tile([P, NHB, HD, 4], BF16, name="vgrp", tag="vgrp", bufs=1, align_bytes=64)
             src = vraw[key][:, NHB * b:NHB * b + NHB].rearrange("p g j d -> p g d j")
             if b == 0:
                 nc.vector.tensor_copy(out=grp[:], in_=src)
@@ -88,14 +121,17 @@ def tile_multiattention_pa_kernel(tc, attn_r, attn_d, v_d, out_rd, out_d):
                                   in_=vgrp[(key, b)][:].rearrange("p g d j -> p (g d j)"))
 
         def quantise(src, tagc, tags):
-            codes = wk.tile([P, 2, N], U32, name=tagc, tag=tagc, align_bytes=64)
-            scales = wk.tile([P, 2, N], U8, name=tags, tag=tags, align_bytes=64)
+            codes = wk.tile([P, 2, N], U32, name=tagc, tag=tagc, bufs=1, align_bytes=64)
+            scales = wk.tile([P, 2, N], U8, name=tags, tag=tags, bufs=1, align_bytes=64)
             nc.vector.quantize_mx(
                 out=codes[:].rearrange("p a n -> p (a n)").bitcast(FP8X4),
                 scales=scales[:].rearrange("p a n -> p (a n)"),
                 in_=src[:].rearrange("p a n t -> p (a n t)"),
             )
             return codes, scales
+
+        def eng_of(g):
+            return ENG_PRO if g < 2 else (ENG_EPI if g >= NH - 1 else ENG)
 
         def ok(g):
             return 0 <= g < NH
@@ -105,23 +141,27 @@ def tile_multiattention_pa_kernel(tc, attn_r, attn_d, v_d, out_rd, out_d):
             st[g] = s
             s["nr"] = ld.tile([P, 4, N], BF16, name="nr", tag="nr")
             nc.sync.dma_start(out=s["nr"][:], in_=wr_v[g])
-            s["nd"] = ld.tile([P, 4, N], BF16, name="nd", tag="nd")
+            s["nd"] = ld.tile([P, 4, N], BF16, name="nd", tag="nd", bufs=5)
             nc.sync.dma_start(out=s["nd"][:], in_=wd_v[g])
 
-        def x4(g):
+        def x4(g, m, t):
             s = st[g]
-            s["x4r"] = wk.tile([P, 4, N], F32, name="x4r", tag="x4r", bufs=3)
-            s["x4d"] = wk.tile([P, 4, N], F32, name="x4d", tag="x4d", bufs=3)
-            s["rs"] = wk.tile([P, 8], F32, name="rs", tag="rs")
-            for m, (dst, src) in enumerate(((s["x4r"], s["nr"]), (s["x4d"], s["nd"]))):
-                for t in range(4):
-                    nc.scalar.activation(out=dst[:, t, :], in_=src[:, t, :], func=ACT.Copy, scale=BETA,
-                                         accum_out=s["rs"][:, 4 * m + t:4 * m + t + 1])
+            if m == 0 and t == 0:
+                s["x4r"] = wk.tile([P, 4, N], F32, name="x4r", tag="x4r", bufs=4)
+                s["x4d"] = wk.tile([P, 4, N], F32, name="x4d", tag="x4d", bufs=4)
+                s["rs"] = wk.tile([P, 8, 8], F32, name="rs", tag="rs", bufs=3)
+            dst, src = ((s["x4r"], s["nr"]), (s["x4d"], s["nd"]))[m]
+            acc = s["rs"][:, 4 * m + t, 0:1]
+            if eng_of(g)["x%d" % (4 * m + t)] == "s":
+                nc.scalar.activation(out=dst[:, t, :], in_=src[:, t, :], func=ACT.Copy, scale=BETA, accum_out=acc)
+            else:
+                nc.vector.tensor_scalar(out=dst[:, t, :], in0=src[:, t, :], scalar1=BETA, scalar2=0.0,
+                                        op0=ALU.mult, op1=ALU.add, accum_out=acc)
 
         def recip(g):
             s = st[g]
             s["inv"] = wk.tile([P, 8], F32, name="inv", tag="inv")
-            nc.vector.reciprocal(out=s["inv"][:], in_=s["rs"][:])
+            nc.vector.reciprocal(out=s["inv"][:], in_=s["rs"][:, :, 0])
 
         def sq(g):
             s = st[g]
@@ -135,7 +175,7 @@ def tile_multiattention_pa_kernel(tc, attn_r, attn_d, v_d, out_rd, out_d):
 
         def dbc(g, m):
             s = st[g]
-            db = ps.tile([P, N], F32, name="dbc", tag="dbc", bufs=2)
+            db = ps.tile([P, N], F32, name="dbc", tag="x", bufs=4)
             for c in range(4):
                 col = s["dr"][:, 4 * m + c:4 * m + c + 1].to_broadcast([P, P])
                 if ("dbc", m, c) in PLAIN:
@@ -144,20 +184,32 @@ def tile_multiattention_pa_kernel(tc, attn_r, attn_d, v_d, out_rd, out_d):
                     nc.tensor.transpose(db[:, P * c:P * c + P], col, ident[:])
             s["dbc%d" % m] = db
 
-        def wkmul(g, m):
+        def wkmul(g, m, t):
             s = st[g]
             src = s["nr"] if m == 0 else s["nd"]
-            w = wk.tile([P, 4, N], F32, name="wk%d" % m, tag="wk%d" % m)
-            for t in range(4):
-                nc.gpsimd.tensor_scalar(out=w[:, t, :], in0=src[:, t, :],
-                                        scalar1=s["dr"][:, 4 * m + t:4 * m + t + 1], scalar2=s["zero"][:, 0:1],
+            if t == 0:
+                s["wk%d" % m] = wk.tile([P, 4, N], F32, name="wk%d" % m, tag="wk%d" % m)
+            w = s["wk%d" % m]
+            col = s["dr"][:, 4 * m + t:4 * m + t + 1]
+            e = eng_of(g)["wk%d" % (4 * m + t)]
+            if e == "g":
+                nc.gpsimd.tensor_scalar(out=w[:, t, :], in0=src[:, t, :], scalar1=col, scalar2=s["zero"][:, 0:1],
                                         op0=ALU.mult, op1=ALU.add)
-            s["wk%d" % m] = w
+            elif e == "v":
+                nc.vector.tensor_scalar(out=w[:, t, :], in0=src[:, t, :], scalar1=col, scalar2=None, op0=ALU.mult)
+            else:
+                nc.scalar.activation(out=w[:, t, :], in_=src[:, t, :], func=ACT.Copy, scale=col)
+
+        def copy_out(g, key, out, in_):
+            if eng_of(g)[key] == "s":
+                nc.scalar.copy(out=out, in_=in_)
+            else:
+                nc.vector.tensor_copy(out=out, in_=in_)
 
         def wdt(g, b2):
             s = st[g]
             if b2 == 0:
-                s["gaw"] = wk.tile([P, 2, N, 4], BF16, name="gaw", tag="gaw", bufs=3, align_bytes=64)
+                s["gaw"] = wk.tile([P, 2, N, 4], BF16, name="gaw", tag="gaw", bufs=2, align_bytes=64)
             nd32 = s["nd"][:].bitcast(F32)
             wt = ps.tile([P, 2, 256], F32, name="wt", tag="misc", bufs=2)
             for ii in range(2):
@@ -169,13 +221,12 @@ def tile_multiattention_pa_kernel(tc, attn_r, attn_d, v_d, out_rd, out_d):
         def wdtc(g, b2):
             s = st[g]
             gd32 = s["gaw"][:, 1].bitcast(F32)
-            nc.scalar.copy(out=gd32[:, 256 * b2:256 * b2 + 256, :],
-                           in_=s["wt%d" % b2][:].rearrange("p u n -> p n u"))
+            copy_out(g, "wd%d" % b2, gd32[:, 256 * b2:256 * b2 + 256, :], s["wt%d" % b2][:].rearrange("p u n -> p n u"))
 
         def tt(g, m):
             s = st[g]
             if m == 0:
-                s["gs"] = wk.tile([P, 2, N, 4], BF16, name="gs", tag="gs", align_bytes=64)
+                s["gs"] = wk.tile([P, 2, N, 4], BF16, name="gs", tag="gs", bufs=1, align_bytes=64)
             gs = s["gs"]
             nc.vector.tensor_tensor(
                 out=gs[:, m].rearrange("p (c i) t -> p c t i", i=4),
@@ -189,7 +240,7 @@ def tile_multiattention_pa_kernel(tc, attn_r, attn_d, v_d, out_rd, out_d):
         def p_pass(g, i):
             s = st[g]
             cs, ss = s["cs"]
-            pp = ps.tile([P, N], F32, name="pp", tag="pp", bufs=2)
+            pp = ps.tile([P, N], F32, name="pp", tag="x", bufs=4)
             nc.tensor.matmul_mx(out=pp[:], lhsT=cs[:, 0, P * i:P * i + P].bitcast(FP8X4),
                                 lhsT_scale=ss[:, 0, P * i:P * i + P],
                                 rhs=cs[:, 1, :].bitcast(FP8X4), rhs_scale=ss[:, 1, :], start=True, stop=True)
@@ -212,7 +263,7 @@ def tile_multiattention_pa_kernel(tc, attn_r, attn_d, v_d, out_rd, out_d):
 
         def at_copy(g, i):
             s = st[g]
-            nc.scalar.copy(out=s["gaw"][:, 0, P * i:P * i + P, :], in_=s["at%d" % i][:].rearrange("p j n -> p n j"))
+            copy_out(g, "at%d" % i, s["gaw"][:, 0, P * i:P * i + P, :], s["at%d" % i][:].rearrange("p j n -> p n j"))
 
         def q_a(g):
             st[g]["ca"] = quantise(st[g]["gaw"], "ca", "sa")
@@ -236,7 +287,7 @@ def tile_multiattention_pa_kernel(tc, attn_r, attn_d, v_d, out_rd, out_d):
             if h == 0:
                 st["o"] = const.tile([P, 2, 4, N], F32, name="obig", tag="obig")
             obig = st["o"]
-            nc.scalar.copy(out=obig[:, :, :, HD * h:HD * h + HD], in_=st[g]["ob"][:])
+            copy_out(g, "oc", obig[:, :, :, HD * h:HD * h + HD], st[g]["ob"][:])
             last = g >= NH - 2
             if last or h % 2 == 1:
                 c0 = HD * h if last else HD * (h - 1)
@@ -245,26 +296,26 @@ def tile_multiattention_pa_kernel(tc, attn_r, attn_d, v_d, out_rd, out_d):
                     nc.sync.dma_start(out=dst[b].rearrange("(i p) c -> p i c", p=P)[:, :, c0:c1],
                                       in_=obig[:, o, :, c0:c1])
 
-        FN = {"load": load, "tt": tt, "dbc": dbc, "q_s": q_s, "p_pass": p_pass, "q_a": q_a, "av": av, "e3": e3,
+        def vreg_s(g, key):
+            if g % 6 == 0 and g < 12:
+                vreg(key, g // 6)
+
+        def q_vs(g, key):
+            if g % 6 == 0 and g < 12:
+                q_v(key, g // 6)
+
+        FN = {"vreg": vreg_s, "q_v": q_vs, "load": load, "tt": tt, "dbc": dbc, "q_s": q_s, "p_pass": p_pass, "q_a": q_a, "av": av, "e3": e3,
               "x4": x4, "ocopy": ocopy, "recip": recip, "sq": sq, "wkmul": wkmul, "at": at, "wdt": wdt,
               "at_copy": at_copy, "wdtc": wdtc, "gate": gate}
-        EXTRA = {(3, "wkmul"): (vreg, "t", 1), (4, "wkmul"): (vreg, "w", 1),
-                 (5, "q_s"): (q_v, "t", 1), (6, "q_s"): (q_v, "w", 1)}
         load(0)
         load(1)
         vload("t")
         load(2)
         vload("w")
-        for key in ("t", "w"):
-            vreg(key, 0)
-            q_v(key, 0)
-        for it in range(-4, NH + 3):
-            for step in STEPS:
+        load(3)
+        for it in range(-5, NH + 3):
+            for step in (STEPS_PRO if it < 1 else (STEPS_EPI if it >= NH - 2 else STEPS)):
                 g = it + step[1]
-                if not ok(g) or (step[0] == "load" and g < 3):
+                if not ok(g) or (step[0] == "load" and g < 4):
                     continue
                 FN[step[0]](g, *step[2:])
-                if step[-1] != 0 or len(step) == 2:
-                    ex = EXTRA.get((it, step[0]))
-                    if ex:
-                        ex[0](*ex[1:])

@@ -1,8 +1,6 @@
 from contextlib import ExitStack
 
-import concourse.bass as bass
 import concourse.mybir as mybir
-import concourse.tile as tile
 from concourse.masks import make_identity
 
 F32 = mybir.dt.float32
@@ -15,307 +13,293 @@ ACT = mybir.ActivationFunctionType
 
 P = 128
 N = 512
+T = N // P
 HD = 64
-NB = 2
 NHB = 8
-NH = NB * NHB
+NH = 16
+VG = 2
 ALPHA = 0.6
 BETA = 0.4
 
 FLOPS = NH * (2 * N * N * N + 2 * 2 * N * N * HD)
 
-ENG = {"wk0": "g", "wk1": "s", "wk2": "g", "wk3": "g", "wk4": "g", "wk5": "g", "wk6": "s", "wk7": "g", "at0": "s", "at1": "s", "at2": "s", "at3": "s", "wd0": "s", "wd1": "s", "oc": "s", "x0": "s", "x1": "s", "x2": "s", "x3": "s", "x4": "s", "x5": "s", "x6": "s", "x7": "s"}
-ENG_PRO = {"wk0": "s", "wk1": "v", "wk2": "g", "wk3": "s", "wk4": "s", "wk5": "s", "wk6": "v", "wk7": "s", "at0": "s", "at1": "s", "at2": "s", "at3": "s", "wd0": "s", "wd1": "s", "oc": "s", "x0": "v", "x1": "s", "x2": "v", "x3": "s", "x4": "v", "x5": "v", "x6": "s", "x7": "s"}
-ENG_EPI = {"wk0": "g", "wk1": "g", "wk2": "s", "wk3": "g", "wk4": "s", "wk5": "g", "wk6": "g", "wk7": "s", "at0": "s", "at1": "v", "at2": "v", "at3": "s", "wd0": "s", "wd1": "s", "oc": "s", "x0": "s", "x1": "s", "x2": "s", "x3": "s", "x4": "s", "x5": "s", "x6": "s", "x7": "s"}
-PLAIN = (
-    ("dbc", 1, 0), ("dbc", 0, 1), ("at", 2, 3), ("at", 3, 3), ("at", 0, 2),
-    ("at", 3, 2), ("at", 2, 1),
-)
-STEPS = (
-    ("q_s", 0), ("vreg", 1, "t"), ("q_v", 1, "t"), ("p_pass", 0, 0), ("q_a", -1),
-    ("p_pass", 0, 1), ("gate", 2), ("p_pass", 0, 2), ("av", -1), ("wkmul", 2, 1, 0),
-    ("e3", 0, 0), ("load", 4), ("wkmul", 2, 1, 3), ("p_pass", 0, 3), ("dbc", 1, 0),
-    ("at", 0, 0), ("e3", 0, 1), ("vreg", 1, "w"), ("e3", 0, 2), ("e3", 0, 3),
-    ("at", 0, 1), ("at_copy", 0, 0), ("ocopy", -1), ("dbc", 1, 1), ("at_copy", 0, 1),
-    ("wkmul", 2, 0, 0), ("wkmul", 2, 1, 1), ("wdt", 1, 0), ("tt", 1, 0), ("at", 0, 3),
-    ("recip", 3), ("wkmul", 2, 1, 2), ("at", 0, 2), ("wkmul", 2, 0, 1), ("tt", 1, 1),
-    ("at_copy", 0, 3), ("x4", 4, 0, 0), ("wdt", 1, 1), ("q_v", 1, "w"), ("at_copy", 0, 2),
-    ("wkmul", 2, 0, 2), ("x4", 4, 1, 0), ("sq", 3), ("wdtc", 1, 0), ("x4", 4, 1, 1),
-    ("x4", 4, 1, 2), ("x4", 4, 0, 1), ("wdtc", 1, 1), ("x4", 4, 0, 2), ("x4", 4, 1, 3),
-    ("wkmul", 2, 0, 3), ("x4", 4, 0, 3),
-)
-STEPS_PRO = (
-    ("q_s", 0), ("p_pass", 0, 0), ("e3", 0, 0), ("gate", 2), ("p_pass", 0, 1),
-    ("wkmul", 2, 0, 0), ("wkmul", 2, 0, 3), ("p_pass", 0, 3), ("dbc", 1, 0), ("e3", 0, 3),
-    ("wkmul", 2, 1, 0), ("e3", 0, 1), ("vreg", 1, "t"), ("p_pass", 0, 2), ("tt", 1, 0),
-    ("q_a", -1), ("at", 0, 0), ("wkmul", 2, 1, 3), ("wkmul", 2, 0, 2), ("e3", 0, 2),
-    ("at", 0, 1), ("ocopy", -1), ("dbc", 1, 1), ("wdt", 1, 1), ("at_copy", 0, 0),
-    ("q_v", 1, "t"), ("tt", 1, 1), ("wkmul", 2, 0, 1), ("at", 0, 3), ("vreg", 1, "w"),
-    ("load", 4), ("at_copy", 0, 1), ("recip", 3), ("at_copy", 0, 3), ("av", -1),
-    ("wkmul", 2, 1, 2), ("at", 0, 2), ("wdt", 1, 0), ("at_copy", 0, 2), ("wdtc", 1, 1),
-    ("x4", 4, 0, 0), ("x4", 4, 0, 1), ("wkmul", 2, 1, 1), ("x4", 4, 0, 2), ("x4", 4, 1, 1),
-    ("x4", 4, 0, 3), ("x4", 4, 1, 3), ("sq", 3), ("x4", 4, 1, 2), ("x4", 4, 1, 0),
-    ("wdtc", 1, 0), ("q_v", 1, "w"),
-)
-STEPS_EPI = (
-    ("wkmul", 2, 0, 3), ("q_s", 0), ("p_pass", 0, 0), ("q_a", -1), ("load", 4),
-    ("p_pass", 0, 1), ("wkmul", 2, 0, 2), ("wdt", 1, 0), ("e3", 0, 0), ("e3", 0, 1),
-    ("x4", 4, 0, 1), ("p_pass", 0, 3), ("q_v", 1, "t"), ("wkmul", 2, 0, 1), ("wdtc", 1, 0),
-    ("wkmul", 2, 1, 0), ("p_pass", 0, 2), ("q_v", 1, "w"), ("e3", 0, 3), ("x4", 4, 1, 0),
-    ("dbc", 1, 0), ("wkmul", 2, 1, 2), ("vreg", 1, "w"), ("at", 0, 0), ("wdt", 1, 1),
-    ("wkmul", 2, 0, 0), ("dbc", 1, 1), ("x4", 4, 1, 3), ("e3", 0, 2), ("at", 0, 1),
-    ("tt", 1, 0), ("tt", 1, 1), ("x4", 4, 0, 3), ("x4", 4, 0, 0), ("at_copy", 0, 0),
-    ("x4", 4, 1, 1), ("at", 0, 3), ("at_copy", 0, 1), ("wkmul", 2, 1, 3), ("at_copy", 0, 3),
-    ("at", 0, 2), ("av", -1), ("sq", 3), ("wdtc", 1, 1), ("at_copy", 0, 2),
-    ("vreg", 1, "t"), ("ocopy", -1), ("recip", 3), ("x4", 4, 0, 2), ("gate", 2),
-    ("x4", 4, 1, 2), ("wkmul", 2, 1, 1),
-)
+WK_SCALAR = ((0, 3), (1, 2), (1, 3))
+WK_VECTOR_FIRST = ((0, 0), (1, 0))
 
 
 def tile_multiattention_pa_kernel(tc, attn_r, attn_d, v_d, out_rd, out_d):
     nc = tc.nc
-    wr_v = attn_r.rearrange("b h (t p) n -> (b h) p t n", p=P)
-    wd_v = attn_d.rearrange("b h (t p) n -> (b h) p t n", p=P)
+    maps = [a.rearrange("b h (t p) n -> (b h) p t n", p=P) for a in (attn_r, attn_d)]
     with ExitStack() as ctx:
         const = ctx.enter_context(tc.tile_pool(name="const", bufs=1))
-        ld = ctx.enter_context(tc.tile_pool(name="ld", bufs=4))
-        wk = ctx.enter_context(tc.tile_pool(name="wk", bufs=2))
+        sb = ctx.enter_context(tc.tile_pool(name="sb", bufs=2))
         ps = ctx.enter_context(tc.psum_pool(name="ps", bufs=1))
-
         ctx.enter_context(tc.manual_schedule())
-        ident = const.tile([P, P], F32, name="ident")
-        make_identity(nc, ident[:])
 
-        vcodes = {}
-        vscales = {}
         st = {}
 
-        vraw = {}
-        vgrp = {}
+        def load(h, pieces):
+            s = {}
+            st[h] = s
+            for m in range(2):
+                s["n%d" % m] = sb.tile([P, T, N], BF16, name="n%d" % m, tag="n%d" % m, bufs=5 + m)
+            w = T // pieces
+            for c in range(pieces):
+                for m in range(2):
+                    nc.sync.dma_start(out=s["n%d" % m][:, w * c:w * c + w, :], in_=maps[m][h][:, w * c:w * c + w, :])
 
-        def vload(key):
-            raw = const.tile([P, NH, 4, HD], BF16, name="vraw_" + key)
-            if key == "t":
-                nc.sync.dma_start(out=raw[:].rearrange("p g j d -> p (g j) d"),
-                                  in_=v_d.rearrange("b h (j p) d -> p (b h j) d", p=P))
+        def rows(h, m, t, vector):
+            s = st[h]
+            if m == 0 and t == 0:
+                s["x0"] = sb.tile([P, T, N], F32, name="x0", tag="x0", bufs=4)
+                s["x1"] = sb.tile([P, T, N], F32, name="x1", tag="x1", bufs=4)
+                s["rs"] = sb.tile([P, 2 * T], F32, name="rs", tag="rs", bufs=3)
+            src = s["n%d" % m][:, t, :]
+            dst = s["x%d" % m][:, t, :]
+            acc = s["rs"][:, T * m + t:T * m + t + 1]
+            if vector:
+                nc.vector.tensor_scalar(out=dst, in0=src, scalar1=BETA, scalar2=0.0, op0=ALU.mult, op1=ALU.add, accum_out=acc)
             else:
-                nc.sync.dma_start(out=raw[:].rearrange("p g (u e) d -> p (g u) (e d)", u=2),
-                                  in_=v_d.rearrange("b h (u p e) d -> p (b h u) (e d)", u=2, e=2))
-            vraw[key] = raw
-            vcodes[key] = const.tile([P, NH * HD], U32, name="vc_" + key, align_bytes=64)
-            vscales[key] = const.tile([P, NH * HD], U8, name="vs_" + key, align_bytes=64)
+                nc.scalar.activation(out=dst, in_=src, func=ACT.Copy, scale=BETA, accum_out=acc)
 
-        def vreg(key, b):
-            grp = const.tile([P, NHB, HD, 4], BF16, name="vgrp", tag="vgrp", bufs=1, align_bytes=64)
-            src = vraw[key][:, NHB * b:NHB * b + NHB].rearrange("p g j d -> p g d j")
-            if b == 0:
-                nc.vector.tensor_copy(out=grp[:], in_=src)
+        def recip(h):
+            s = st[h]
+            s["inv"] = sb.tile([P, 2 * T], F32, name="inv", tag="inv")
+            nc.vector.reciprocal(out=s["inv"][:], in_=s["rs"][:])
+            s["zero"] = sb.tile([P, 2 * T], F32, name="zero", tag="zero")
+            nc.vector.memset(s["zero"][:], 0.0)
+
+        def root(h):
+            s = st[h]
+            s["d"] = sb.tile([P, 2 * T], F32, name="d", tag="d", bufs=3)
+            nc.scalar.activation(out=s["d"][:], in_=s["inv"][:], func=ACT.Sqrt, scale=BETA)
+
+        def wk_engine(h, m, t):
+            if h == 0 and (m, t) in WK_VECTOR_FIRST:
+                return "v"
+            return "s" if (m, t) in WK_SCALAR else "g"
+
+        def wk(h, m, t):
+            s = st[h]
+            if "wk" not in s:
+                s["wk"] = [sb.tile([P, T, N], F32, name="wk%d" % i, tag="wk%d" % i, bufs=2) for i in range(2)]
+            src = s["n%d" % m][:, t, :]
+            dst = s["wk"][m][:, t, :]
+            col = s["d"][:, T * m + t:T * m + t + 1]
+            e = wk_engine(h, m, t)
+            if e == "g":
+                nc.gpsimd.tensor_scalar(out=dst, in0=src, scalar1=col, scalar2=s["zero"][:, 0:1], op0=ALU.mult, op1=ALU.add)
+            elif e == "v":
+                nc.vector.tensor_scalar(out=dst, in0=src, scalar1=col, scalar2=None, op0=ALU.mult)
             else:
-                nc.gpsimd.tensor_scalar(out=grp[:], in0=src, scalar1=1.0, scalar2=0.0, op0=ALU.mult, op1=ALU.add)
-            vgrp[(key, b)] = grp
+                nc.scalar.activation(out=dst, in_=src, func=ACT.Copy, scale=col)
 
-        def q_v(key, b):
-            w = NHB * HD
-            nc.vector.quantize_mx(out=vcodes[key][:, w * b:w * b + w].bitcast(FP8X4),
-                                  scales=vscales[key][:, w * b:w * b + w],
-                                  in_=vgrp[(key, b)][:].rearrange("p g d j -> p (g d j)"))
+        def xadd(h, t):
+            s = st[h]
+            nc.gpsimd.tensor_tensor(out=s["x0"][:, t, :], in0=s["x0"][:, t, :], in1=s["x1"][:, t, :], op=ALU.add)
 
-        def quantise(src, tagc, tags):
-            codes = wk.tile([P, 2, N], U32, name=tagc, tag=tagc, bufs=1, align_bytes=64)
-            scales = wk.tile([P, 2, N], U8, name=tags, tag=tags, bufs=1, align_bytes=64)
+        def dbc(h, m):
+            s = st[h]
+            db = ps.tile([P, N], F32, name="dbc", tag="dbc", bufs=1)
+            for c in range(T):
+                col = s["d"][:, T * m + c:T * m + c + 1].to_broadcast([P, P])
+                nc.tensor.transpose(db[:, P * c:P * c + P], col, ident[:])
+            s["dbc"] = db
+
+        def cols(h, m):
+            s = st[h]
+            if m == 0:
+                s["gs"] = sb.tile([P, 2, N, 4], BF16, name="gs", tag="gs", bufs=2, align_bytes=64)
+            nc.vector.tensor_tensor(
+                out=s["gs"][:, m].rearrange("p (c i) t -> p c t i", i=4),
+                in0=s["wk"][m][:].rearrange("p t (c i) -> p c t i", i=4),
+                in1=s["dbc"][:].rearrange("p (c i) -> p c i", i=4).unsqueeze(2).to_broadcast([P, N // 4, 4, 4]),
+                op=ALU.mult)
+
+        def quantise(src, tag):
+            codes = sb.tile([P, 2, N], U32, name="c" + tag, tag="c" + tag, bufs=2, align_bytes=64)
+            scales = sb.tile([P, 2, N], U8, name="s" + tag, tag="s" + tag, bufs=2, align_bytes=64)
             nc.vector.quantize_mx(
                 out=codes[:].rearrange("p a n -> p (a n)").bitcast(FP8X4),
                 scales=scales[:].rearrange("p a n -> p (a n)"),
-                in_=src[:].rearrange("p a n t -> p (a n t)"),
-            )
+                in_=src[:].rearrange("p a n t -> p (a n t)"))
             return codes, scales
 
-        def eng_of(g):
-            return ENG_PRO if g < 2 else (ENG_EPI if g >= NH - 1 else ENG)
+        def q_s(h):
+            st[h]["cs"] = quantise(st[h]["gs"], "s")
 
-        def ok(g):
-            return 0 <= g < NH
+        def q_a(h):
+            st[h]["ca"] = quantise(st[h]["gaw"], "a")
 
-        def load(g):
-            s = {}
-            st[g] = s
-            s["nr"] = ld.tile([P, 4, N], BF16, name="nr", tag="nr")
-            nc.sync.dma_start(out=s["nr"][:], in_=wr_v[g])
-            s["nd"] = ld.tile([P, 4, N], BF16, name="nd", tag="nd", bufs=5)
-            nc.sync.dma_start(out=s["nd"][:], in_=wd_v[g])
-
-        def x4(g, m, t):
-            s = st[g]
-            if m == 0 and t == 0:
-                s["x4r"] = wk.tile([P, 4, N], F32, name="x4r", tag="x4r", bufs=4)
-                s["x4d"] = wk.tile([P, 4, N], F32, name="x4d", tag="x4d", bufs=4)
-                s["rs"] = wk.tile([P, 8, 8], F32, name="rs", tag="rs", bufs=3)
-            dst, src = ((s["x4r"], s["nr"]), (s["x4d"], s["nd"]))[m]
-            acc = s["rs"][:, 4 * m + t, 0:1]
-            if eng_of(g)["x%d" % (4 * m + t)] == "s":
-                nc.scalar.activation(out=dst[:, t, :], in_=src[:, t, :], func=ACT.Copy, scale=BETA, accum_out=acc)
-            else:
-                nc.vector.tensor_scalar(out=dst[:, t, :], in0=src[:, t, :], scalar1=BETA, scalar2=0.0,
-                                        op0=ALU.mult, op1=ALU.add, accum_out=acc)
-
-        def recip(g):
-            s = st[g]
-            s["inv"] = wk.tile([P, 8], F32, name="inv", tag="inv")
-            nc.vector.reciprocal(out=s["inv"][:], in_=s["rs"][:, :, 0])
-
-        def sq(g):
-            s = st[g]
-            inv = s["inv"]
-            s["dr"] = wk.tile([P, 8], F32, name="dr", tag="dr")
-            nc.scalar.activation(out=s["dr"][:], in_=inv[:], func=ACT.Sqrt, scale=BETA)
-
-        def gate(g):
-            st[g]["zero"] = wk.tile([P, 8], F32, name="zero", tag="zero")
-            nc.vector.memset(st[g]["zero"][:], 0.0)
-
-        def dbc(g, m):
-            s = st[g]
-            db = ps.tile([P, N], F32, name="dbc", tag="x", bufs=4)
-            for c in range(4):
-                col = s["dr"][:, 4 * m + c:4 * m + c + 1].to_broadcast([P, P])
-                if ("dbc", m, c) in PLAIN:
-                    nc.tensor.matmul(out=db[:, P * c:P * c + P], lhsT=col, rhs=ident[:], start=True, stop=True)
-                else:
-                    nc.tensor.transpose(db[:, P * c:P * c + P], col, ident[:])
-            s["dbc%d" % m] = db
-
-        def wkmul(g, m, t):
-            s = st[g]
-            src = s["nr"] if m == 0 else s["nd"]
-            if t == 0:
-                s["wk%d" % m] = wk.tile([P, 4, N], F32, name="wk%d" % m, tag="wk%d" % m)
-            w = s["wk%d" % m]
-            col = s["dr"][:, 4 * m + t:4 * m + t + 1]
-            e = eng_of(g)["wk%d" % (4 * m + t)]
-            if e == "g":
-                nc.gpsimd.tensor_scalar(out=w[:, t, :], in0=src[:, t, :], scalar1=col, scalar2=s["zero"][:, 0:1],
-                                        op0=ALU.mult, op1=ALU.add)
-            elif e == "v":
-                nc.vector.tensor_scalar(out=w[:, t, :], in0=src[:, t, :], scalar1=col, scalar2=None, op0=ALU.mult)
-            else:
-                nc.scalar.activation(out=w[:, t, :], in_=src[:, t, :], func=ACT.Copy, scale=col)
-
-        def copy_out(g, key, out, in_):
-            if eng_of(g)[key] == "s":
-                nc.scalar.copy(out=out, in_=in_)
-            else:
-                nc.vector.tensor_copy(out=out, in_=in_)
-
-        def wdt(g, b2):
-            s = st[g]
-            if b2 == 0:
-                s["gaw"] = wk.tile([P, 2, N, 4], BF16, name="gaw", tag="gaw", bufs=2, align_bytes=64)
-            nd32 = s["nd"][:].bitcast(F32)
-            wt = ps.tile([P, 2, 256], F32, name="wt", tag="misc", bufs=2)
-            for ii in range(2):
-                for u in range(2):
-                    nc.tensor.transpose(wt[:, u, P * ii:P * ii + P],
-                                        nd32[:, 2 * b2 + ii, P * u:P * u + P], ident[:])
-            s["wt%d" % b2] = wt
-
-        def wdtc(g, b2):
-            s = st[g]
-            gd32 = s["gaw"][:, 1].bitcast(F32)
-            copy_out(g, "wd%d" % b2, gd32[:, 256 * b2:256 * b2 + 256, :], s["wt%d" % b2][:].rearrange("p u n -> p n u"))
-
-        def tt(g, m):
-            s = st[g]
-            if m == 0:
-                s["gs"] = wk.tile([P, 2, N, 4], BF16, name="gs", tag="gs", bufs=1, align_bytes=64)
-            gs = s["gs"]
-            nc.vector.tensor_tensor(
-                out=gs[:, m].rearrange("p (c i) t -> p c t i", i=4),
-                in0=s["wk%d" % m][:].rearrange("p t (c i) -> p c t i", i=4),
-                in1=s["dbc%d" % m][:].rearrange("p (c i) -> p c i", i=4).unsqueeze(2).to_broadcast([P, N // 4, 4, 4]),
-                op=ALU.mult)
-
-        def q_s(g):
-            st[g]["cs"] = quantise(st[g]["gs"], "cs", "ss")
-
-        def p_pass(g, i):
-            s = st[g]
-            cs, ss = s["cs"]
-            pp = ps.tile([P, N], F32, name="pp", tag="x", bufs=4)
-            nc.tensor.matmul_mx(out=pp[:], lhsT=cs[:, 0, P * i:P * i + P].bitcast(FP8X4),
-                                lhsT_scale=ss[:, 0, P * i:P * i + P],
-                                rhs=cs[:, 1, :].bitcast(FP8X4), rhs_scale=ss[:, 1, :], start=True, stop=True)
+        def pmul(h, i):
+            s = st[h]
+            codes, scales = s["cs"]
+            pp = ps.tile([P, N], F32, name="pp", tag="pp", bufs=4)
+            nc.tensor.matmul_mx(out=pp[:], lhsT=codes[:, 0, P * i:P * i + P].bitcast(FP8X4),
+                                lhsT_scale=scales[:, 0, P * i:P * i + P],
+                                rhs=codes[:, 1, :].bitcast(FP8X4), rhs_scale=scales[:, 1, :], start=True, stop=True)
             s["pp%d" % i] = pp
 
-        def e3(g, i):
-            s = st[g]
-            nc.vector.scalar_tensor_tensor(out=s["x4r"][:, i, :], in0=s["pp%d" % i][:], scalar=ALPHA,
-                                           in1=s["x4r"][:, i, :], op0=ALU.mult, op1=ALU.add)
+        def amix(h, i):
+            s = st[h]
+            if i == 0:
+                s["a"] = sb.tile([P, T, N], BF16, name="a", tag="a", bufs=2)
+            nc.vector.scalar_tensor_tensor(out=s["a"][:, i, :], in0=s["pp%d" % i][:], scalar=ALPHA,
+                                           in1=s["x0"][:, i, :], op0=ALU.mult, op1=ALU.add)
 
-        def at(g, i):
-            s = st[g]
-            a = ps.tile([P, 4, P], F32, name="at", tag="at", bufs=2)
-            for j in range(4):
-                nc.tensor.matmul(out=a[:, j, :], lhsT=s["x4r"][:, i, P * j:P * j + P], rhs=ident[:],
-                                 is_transpose=True, start=True, stop=False)
-                nc.tensor.matmul(out=a[:, j, :], lhsT=s["x4d"][:, i, P * j:P * j + P], rhs=ident[:],
-                                 is_transpose=(("at", i, j) not in PLAIN), start=False, stop=True)
-            s["at%d" % i] = a
+        def turn(h, o, b2):
+            s = st[h]
+            if "gaw" not in s:
+                s["gaw"] = sb.tile([P, 2, N, 4], BF16, name="gaw", tag="gaw", bufs=2, align_bytes=64)
+            words = s["a" if o == 0 else "n1"][:].bitcast(F32)
+            tw = ps.tile([P, 2, 256], F32, name="tw", tag="tw", bufs=3)
+            for ii in range(2):
+                for u in range(2):
+                    nc.tensor.transpose(tw[:, u, P * ii:P * ii + P], words[:, 2 * b2 + ii, P * u:P * u + P], ident[:])
+            s["tw%d%d" % (o, b2)] = tw
 
-        def at_copy(g, i):
-            s = st[g]
-            copy_out(g, "at%d" % i, s["gaw"][:, 0, P * i:P * i + P, :], s["at%d" % i][:].rearrange("p j n -> p n j"))
+        def turn_copy(h, o, b2):
+            s = st[h]
+            g32 = s["gaw"][:, o].bitcast(F32)
+            nc.scalar.copy(out=g32[:, 256 * b2:256 * b2 + 256, :], in_=s["tw%d%d" % (o, b2)][:].rearrange("p u n -> p n u"))
 
-        def q_a(g):
-            st[g]["ca"] = quantise(st[g]["gaw"], "ca", "sa")
-
-        def av(g):
-            s = st[g]
-            ob = ps.tile([P, 2, 4, HD], F32, name="ob", tag="misc", bufs=2)
-            for o, key in enumerate(("t", "w")):
-                cc, ss = s["ca"]
-                for i in range(4):
-                    nc.tensor.matmul_mx(out=ob[:, o, i, :], lhsT=cc[:, o, P * i:P * i + P].bitcast(FP8X4),
-                                        lhsT_scale=ss[:, o, P * i:P * i + P],
-                                        rhs=vcodes[key][:, HD * g:HD * g + HD].bitcast(FP8X4),
-                                        rhs_scale=vscales[key][:, HD * g:HD * g + HD],
+        def av(h):
+            s = st[h]
+            codes, scales = s["ca"]
+            vc, vs = st["v%d" % (h // VG)]
+            c0 = HD * (h % VG)
+            ob = ps.tile([P, 2, T, HD], F32, name="ob", tag="tw", bufs=3)
+            for o in range(2):
+                for i in range(T):
+                    nc.tensor.matmul_mx(out=ob[:, o, i, :], lhsT=codes[:, o, P * i:P * i + P].bitcast(FP8X4),
+                                        lhsT_scale=scales[:, o, P * i:P * i + P],
+                                        rhs=vc[:, c0:c0 + HD].bitcast(FP8X4), rhs_scale=vs[:, c0:c0 + HD],
                                         start=True, stop=True)
             s["ob"] = ob
 
-        def ocopy(g):
-            b = g // NHB
-            h = g % NHB
-            if h == 0:
-                st["o"] = const.tile([P, 2, 4, N], F32, name="obig", tag="obig")
-            obig = st["o"]
-            copy_out(g, "oc", obig[:, :, :, HD * h:HD * h + HD], st[g]["ob"][:])
-            last = g >= NH - 2
-            if last or h % 2 == 1:
-                c0 = HD * h if last else HD * (h - 1)
-                c1 = HD * (h + 1)
+        def ocopy(h):
+            b = h // NHB
+            k = h % NHB
+            q = k % 2
+            if q == 0:
+                st["o"] = sb.tile([P, 2, T, 2 * HD], F32, name="o", tag="o", bufs=3)
+            ot = st["o"]
+            nc.scalar.copy(out=ot[:, :, :, HD * q:HD * q + HD], in_=st[h]["ob"][:])
+            last = h >= NH - 2
+            if last or q == 1:
+                q0 = q if last else 0
+                c0 = HD * (k - q + q0)
+                w = HD * (q + 1 - q0)
                 for o, dst in enumerate((out_rd, out_d)):
-                    nc.sync.dma_start(out=dst[b].rearrange("(i p) c -> p i c", p=P)[:, :, c0:c1],
-                                      in_=obig[:, o, :, c0:c1])
+                    nc.sync.dma_start(out=dst[b].rearrange("(i p) c -> p i c", p=P)[:, :, c0:c0 + w],
+                                      in_=ot[:, o, :, HD * q0:HD * q0 + w])
 
-        def vreg_s(g, key):
-            if g % 6 == 0 and g < 12:
-                vreg(key, g // 6)
+        def vgroup(v):
+            grp = sb.tile([P, VG, HD, 4], BF16, name="vgrp", tag="vgrp", bufs=2, align_bytes=64)
+            nc.gpsimd.tensor_scalar(out=grp[:], in0=vraw[:, VG * v:VG * v + VG].rearrange("p g j d -> p g d j"),
+                                    scalar1=1.0, scalar2=0.0, op0=ALU.mult, op1=ALU.add)
+            st["vg%d" % v] = grp
 
-        def q_vs(g, key):
-            if g % 6 == 0 and g < 12:
-                q_v(key, g // 6)
+        def q_v(v):
+            codes = sb.tile([P, VG * HD], U32, name="cv", tag="cv", bufs=2, align_bytes=64)
+            scales = sb.tile([P, VG * HD], U8, name="sv", tag="sv", bufs=2, align_bytes=64)
+            nc.vector.quantize_mx(out=codes[:].bitcast(FP8X4), scales=scales[:],
+                                  in_=st["vg%d" % v][:].rearrange("p g d j -> p (g d j)"))
+            st["v%d" % v] = (codes, scales)
 
-        FN = {"vreg": vreg_s, "q_v": q_vs, "load": load, "tt": tt, "dbc": dbc, "q_s": q_s, "p_pass": p_pass, "q_a": q_a, "av": av, "e3": e3,
-              "x4": x4, "ocopy": ocopy, "recip": recip, "sq": sq, "wkmul": wkmul, "at": at, "wdt": wdt,
-              "at_copy": at_copy, "wdtc": wdtc, "gate": gate}
-        load(0)
-        load(1)
-        vload("t")
-        load(2)
-        vload("w")
-        load(3)
-        for it in range(-5, NH + 3):
-            for step in (STEPS_PRO if it < 1 else (STEPS_EPI if it >= NH - 2 else STEPS)):
-                g = it + step[1]
-                if not ok(g) or (step[0] == "load" and g < 4):
-                    continue
-                FN[step[0]](g, *step[2:])
+        zero = const.tile([P, 8], F32, name="warm")
+        nc.vector.memset(zero[:], 0.0)
+        warm = const.tile([P, 8], F32, name="warm_out")
+        nc.scalar.activation(out=warm[:], in_=zero[:], func=ACT.Sqrt)
+        load(0, T)
+        ident = const.tile([P, P], F32, name="ident")
+        make_identity(nc, ident[:])
+        load(1, 1)
+        vraw = const.tile([P, NH, 4, HD], BF16, name="vraw")
+        nc.sync.dma_start(out=vraw[:].rearrange("p g (u e) d -> p (g u) (e d)", u=2),
+                          in_=v_d.rearrange("b h (u p e) d -> p (b h u) (e d)", u=2, e=2))
+        load(2, 1)
+        load(3, 1)
+
+        tiles = [(m, t) for m in range(2) for t in range(T)]
+        for it in range(-3, NH + 1):
+            new = it + 3
+            scl = it + 2
+            nxt = it + 1
+            cur = it
+            old = it - 1
+
+            def on(h):
+                return 0 <= h < NH
+
+            if on(it + 4) and it + 4 > 3:
+                load(it + 4, 1)
+            if on(cur):
+                q_s(cur)
+            if on(nxt):
+                dbc(nxt, 0)
+            if on(cur):
+                for i in range(T):
+                    pmul(cur, i)
+            if on(old):
+                if old % VG == 0:
+                    q_v(old // VG)
+                q_a(old)
+            late = []
+            more = []
+            if it < 0:
+                if on(scl):
+                    recip(scl)
+                    root(scl)
+                    for m, t in tiles:
+                        wk(scl, m, t)
+                for m, t in tiles:
+                    rows(new, m, t, new < 2 and t % 2 == 1)
+            else:
+                if on(new):
+                    for m, t in tiles[:4]:
+                        rows(new, m, t, False)
+                    more = tiles[4:]
+                if on(scl):
+                    recip(scl)
+                    root(scl)
+                    for m, t in tiles:
+                        if wk_engine(scl, m, t) == "s":
+                            late.append((m, t))
+                        else:
+                            wk(scl, m, t)
+            if on(old):
+                av(old)
+            if on(nxt):
+                cols(nxt, 0)
+            if late:
+                wk(scl, *late.pop(0))
+            if more:
+                rows(new, *more.pop(0), False)
+            if on(old):
+                ocopy(old)
+            if on(nxt):
+                for b2 in range(2):
+                    turn(nxt, 1, b2)
+                    turn_copy(nxt, 1, b2)
+                dbc(nxt, 1)
+            if late:
+                wk(scl, *late.pop(0))
+            if more:
+                rows(new, *more.pop(0), False)
+            for b2 in range(2):
+                if on(cur):
+                    amix(cur, 2 * b2)
+                    amix(cur, 2 * b2 + 1)
+                    turn(cur, 0, b2)
+                    turn_copy(cur, 0, b2)
+                if more:
+                    rows(new, *more.pop(0), False)
+            for m, t in late:
+                wk(scl, m, t)
+            if on(nxt):
+                cols(nxt, 1)
+                for t in range(T):
+                    xadd(nxt, t)
+                if nxt % VG == 0:
+                    vgroup(nxt // VG)

@@ -23,7 +23,8 @@ BETA = 0.4
 
 FLOPS = NH * (2 * N * N * N + 2 * 2 * N * N * HD)
 
-WK_SCALAR = ((0, 3), (1, 2), (1, 3))
+WK_SCALAR = ((1, 3),)
+PLAIN = 7
 WK_VECTOR_FIRST = ((0, 0), (1, 0))
 
 
@@ -75,8 +76,8 @@ def tile_multiattention_pa_kernel(tc, attn_r, attn_d, v_d, out_rd, out_d):
             nc.scalar.activation(out=s["d"][:], in_=s["inv"][:], func=ACT.Sqrt, scale=BETA)
 
         def wk_engine(h, m, t):
-            if h == 0 and (m, t) in WK_VECTOR_FIRST:
-                return "v"
+            if h == 0:
+                return "v" if (m, t) in WK_VECTOR_FIRST else ("s" if t >= 2 and m == 1 else "g")
             return "s" if (m, t) in WK_SCALAR else "g"
 
         def wk(h, m, t):
@@ -94,16 +95,15 @@ def tile_multiattention_pa_kernel(tc, attn_r, attn_d, v_d, out_rd, out_d):
             else:
                 nc.scalar.activation(out=dst, in_=src, func=ACT.Copy, scale=col)
 
-        def xadd(h, t):
-            s = st[h]
-            nc.gpsimd.tensor_tensor(out=s["x0"][:, t, :], in0=s["x0"][:, t, :], in1=s["x1"][:, t, :], op=ALU.add)
-
         def dbc(h, m):
             s = st[h]
             db = ps.tile([P, N], F32, name="dbc", tag="dbc", bufs=1)
             for c in range(T):
                 col = s["d"][:, T * m + c:T * m + c + 1].to_broadcast([P, P])
-                nc.tensor.transpose(db[:, P * c:P * c + P], col, ident[:])
+                if T * m + c < PLAIN:
+                    nc.tensor.matmul(out=db[:, P * c:P * c + P], lhsT=col, rhs=ident[:], start=True, stop=True)
+                else:
+                    nc.tensor.transpose(db[:, P * c:P * c + P], col, ident[:])
             s["dbc"] = db
 
         def cols(h, m):
@@ -142,16 +142,27 @@ def tile_multiattention_pa_kernel(tc, attn_r, attn_d, v_d, out_rd, out_d):
 
         def amix(h, i):
             s = st[h]
-            if i == 0:
-                s["a"] = sb.tile([P, T, N], BF16, name="a", tag="a", bufs=2)
-            nc.vector.scalar_tensor_tensor(out=s["a"][:, i, :], in0=s["pp%d" % i][:], scalar=ALPHA,
+            nc.vector.scalar_tensor_tensor(out=s["x0"][:, i, :], in0=s["pp%d" % i][:], scalar=ALPHA,
                                            in1=s["x0"][:, i, :], op0=ALU.mult, op1=ALU.add)
+
+        def aturn(h, i):
+            s = st[h]
+            at = ps.tile([P, T, P], F32, name="at", tag="tw", bufs=3)
+            for j in range(T):
+                for m in range(2):
+                    nc.tensor.matmul(out=at[:, j, :], lhsT=s["x%d" % m][:, i, P * j:P * j + P], rhs=ident[:],
+                                     is_transpose=True, start=m == 0, stop=m == 1)
+            s["at%d" % i] = at
+
+        def acopy(h, i):
+            s = st[h]
+            nc.scalar.copy(out=s["gaw"][:, 0, P * i:P * i + P, :], in_=s["at%d" % i][:].rearrange("p j n -> p n j"))
 
         def turn(h, o, b2):
             s = st[h]
-            if "gaw" not in s:
+            if b2 == 0:
                 s["gaw"] = sb.tile([P, 2, N, 4], BF16, name="gaw", tag="gaw", bufs=2, align_bytes=64)
-            words = s["a" if o == 0 else "n1"][:].bitcast(F32)
+            words = s["n1"][:].bitcast(F32)
             tw = ps.tile([P, 2, 256], F32, name="tw", tag="tw", bufs=3)
             for ii in range(2):
                 for u in range(2):
@@ -166,10 +177,10 @@ def tile_multiattention_pa_kernel(tc, attn_r, attn_d, v_d, out_rd, out_d):
         def av(h):
             s = st[h]
             codes, scales = s["ca"]
-            vc, vs = st["v%d" % (h // VG)]
             c0 = HD * (h % VG)
             ob = ps.tile([P, 2, T, HD], F32, name="ob", tag="tw", bufs=3)
             for o in range(2):
+                vc, vs = st["v%d%d" % (o, h // VG)]
                 for i in range(T):
                     nc.tensor.matmul_mx(out=ob[:, o, i, :], lhsT=codes[:, o, P * i:P * i + P].bitcast(FP8X4),
                                         lhsT_scale=scales[:, o, P * i:P * i + P],
@@ -195,17 +206,19 @@ def tile_multiattention_pa_kernel(tc, attn_r, attn_d, v_d, out_rd, out_d):
                                       in_=ot[:, o, :, HD * q0:HD * q0 + w])
 
         def vgroup(v):
-            grp = sb.tile([P, VG, HD, 4], BF16, name="vgrp", tag="vgrp", bufs=2, align_bytes=64)
-            nc.gpsimd.tensor_scalar(out=grp[:], in0=vraw[:, VG * v:VG * v + VG].rearrange("p g j d -> p g d j"),
-                                    scalar1=1.0, scalar2=0.0, op0=ALU.mult, op1=ALU.add)
-            st["vg%d" % v] = grp
+            for o in range(2):
+                grp = sb.tile([P, VG, HD, 4], BF16, name="vgrp", tag="vgrp", bufs=4, align_bytes=64)
+                nc.gpsimd.tensor_scalar(out=grp[:], in0=vraw[o][:, VG * v:VG * v + VG].rearrange("p g j d -> p g d j"),
+                                        scalar1=1.0, scalar2=0.0, op0=ALU.mult, op1=ALU.add)
+                st["vg%d%d" % (o, v)] = grp
 
         def q_v(v):
-            codes = sb.tile([P, VG * HD], U32, name="cv", tag="cv", bufs=2, align_bytes=64)
-            scales = sb.tile([P, VG * HD], U8, name="sv", tag="sv", bufs=2, align_bytes=64)
-            nc.vector.quantize_mx(out=codes[:].bitcast(FP8X4), scales=scales[:],
-                                  in_=st["vg%d" % v][:].rearrange("p g d j -> p (g d j)"))
-            st["v%d" % v] = (codes, scales)
+            for o in range(2):
+                codes = sb.tile([P, VG * HD], U32, name="cv", tag="cv", bufs=4, align_bytes=64)
+                scales = sb.tile([P, VG * HD], U8, name="sv", tag="sv", bufs=4, align_bytes=64)
+                nc.vector.quantize_mx(out=codes[:].bitcast(FP8X4), scales=scales[:],
+                                      in_=st["vg%d%d" % (o, v)][:].rearrange("p g d j -> p (g d j)"))
+                st["v%d%d" % (o, v)] = (codes, scales)
 
         zero = const.tile([P, 8], F32, name="warm")
         nc.vector.memset(zero[:], 0.0)
@@ -215,10 +228,15 @@ def tile_multiattention_pa_kernel(tc, attn_r, attn_d, v_d, out_rd, out_d):
         ident = const.tile([P, P], F32, name="ident")
         make_identity(nc, ident[:])
         load(1, 1)
-        vraw = const.tile([P, NH, 4, HD], BF16, name="vraw")
-        nc.sync.dma_start(out=vraw[:].rearrange("p g (u e) d -> p (g u) (e d)", u=2),
-                          in_=v_d.rearrange("b h (u p e) d -> p (b h u) (e d)", u=2, e=2))
         load(2, 1)
+        vraw = []
+        for o in range(2):
+            raw = const.tile([P, NH, 4, HD], BF16, name="vraw%d" % o)
+            vraw.append(raw)
+        nc.sync.dma_start(out=vraw[0][:].rearrange("p g j d -> p (g j) d"),
+                          in_=v_d.rearrange("b h (j p) d -> p (b h j) d", p=P))
+        nc.sync.dma_start(out=vraw[1][:].rearrange("p g (u e) d -> p (g u) (e d)", u=2),
+                          in_=v_d.rearrange("b h (u p e) d -> p (b h u) (e d)", u=2, e=2))
         load(3, 1)
 
         tiles = [(m, t) for m in range(2) for t in range(T)]
@@ -272,8 +290,6 @@ def tile_multiattention_pa_kernel(tc, attn_r, attn_d, v_d, out_rd, out_d):
                 av(old)
             if on(nxt):
                 cols(nxt, 0)
-            if late:
-                wk(scl, *late.pop(0))
             if more:
                 rows(new, *more.pop(0), False)
             if on(old):
@@ -283,23 +299,18 @@ def tile_multiattention_pa_kernel(tc, attn_r, attn_d, v_d, out_rd, out_d):
                     turn(nxt, 1, b2)
                     turn_copy(nxt, 1, b2)
                 dbc(nxt, 1)
-            if late:
-                wk(scl, *late.pop(0))
             if more:
                 rows(new, *more.pop(0), False)
-            for b2 in range(2):
-                if on(cur):
-                    amix(cur, 2 * b2)
-                    amix(cur, 2 * b2 + 1)
-                    turn(cur, 0, b2)
-                    turn_copy(cur, 0, b2)
-                if more:
-                    rows(new, *more.pop(0), False)
+            if on(cur):
+                for i in range(T):
+                    amix(cur, i)
+                    aturn(cur, i)
+                    acopy(cur, i)
+            for m, t in more:
+                rows(new, m, t, False)
             for m, t in late:
                 wk(scl, m, t)
             if on(nxt):
                 cols(nxt, 1)
-                for t in range(T):
-                    xadd(nxt, t)
                 if nxt % VG == 0:
                     vgroup(nxt // VG)

@@ -17,15 +17,14 @@ T = N // P
 HD = 64
 NHB = 8
 NH = 16
-VG = 2
 ALPHA = 0.6
 BETA = 0.4
 
 FLOPS = NH * (2 * N * N * N + 2 * 2 * N * N * HD)
 
 WK_SCALAR = ((1, 3),)
+WK_VECTOR = ((0, 0), (1, 0))
 PLAIN = 7
-WK_VECTOR_FIRST = ((0, 0), (1, 0))
 
 
 def tile_multiattention_pa_kernel(tc, attn_r, attn_d, v_d, out_rd, out_d):
@@ -67,6 +66,9 @@ def tile_multiattention_pa_kernel(tc, attn_r, attn_d, v_d, out_rd, out_d):
             s = st[h]
             s["inv"] = sb.tile([P, 2 * T], F32, name="inv", tag="inv")
             nc.vector.reciprocal(out=s["inv"][:], in_=s["rs"][:])
+
+        def gate(h):
+            s = st[h]
             s["zero"] = sb.tile([P, 2 * T], F32, name="zero", tag="zero")
             nc.vector.memset(s["zero"][:], 0.0)
 
@@ -77,7 +79,9 @@ def tile_multiattention_pa_kernel(tc, attn_r, attn_d, v_d, out_rd, out_d):
 
         def wk_engine(h, m, t):
             if h == 0:
-                return "v" if (m, t) in WK_VECTOR_FIRST else ("s" if t >= 2 and m == 1 else "g")
+                return "s" if t == T - 1 else "v"
+            if (m, t) in WK_VECTOR:
+                return "v"
             return "s" if (m, t) in WK_SCALAR else "g"
 
         def wk(h, m, t):
@@ -100,7 +104,7 @@ def tile_multiattention_pa_kernel(tc, attn_r, attn_d, v_d, out_rd, out_d):
             db = ps.tile([P, N], F32, name="dbc", tag="dbc", bufs=1)
             for c in range(T):
                 col = s["d"][:, T * m + c:T * m + c + 1].to_broadcast([P, P])
-                if T * m + c < PLAIN:
+                if h > 0 and T * m + c < PLAIN:
                     nc.tensor.matmul(out=db[:, P * c:P * c + P], lhsT=col, rhs=ident[:], start=True, stop=True)
                 else:
                     nc.tensor.transpose(db[:, P * c:P * c + P], col, ident[:])
@@ -109,7 +113,7 @@ def tile_multiattention_pa_kernel(tc, attn_r, attn_d, v_d, out_rd, out_d):
         def cols(h, m):
             s = st[h]
             if m == 0:
-                s["gs"] = sb.tile([P, 2, N, 4], BF16, name="gs", tag="gs", bufs=2, align_bytes=64)
+                s["gs"] = sb.tile([P, 2, N, 4], BF16, name="gs", tag="gs", bufs=1, align_bytes=64)
             nc.vector.tensor_tensor(
                 out=s["gs"][:, m].rearrange("p (c i) t -> p c t i", i=4),
                 in0=s["wk"][m][:].rearrange("p t (c i) -> p c t i", i=4),
@@ -117,8 +121,8 @@ def tile_multiattention_pa_kernel(tc, attn_r, attn_d, v_d, out_rd, out_d):
                 op=ALU.mult)
 
         def quantise(src, tag):
-            codes = sb.tile([P, 2, N], U32, name="c" + tag, tag="c" + tag, bufs=2, align_bytes=64)
-            scales = sb.tile([P, 2, N], U8, name="s" + tag, tag="s" + tag, bufs=2, align_bytes=64)
+            codes = sb.tile([P, 2, N], U32, name="c" + tag, tag="c" + tag, bufs=1, align_bytes=64)
+            scales = sb.tile([P, 2, N], U8, name="s" + tag, tag="s" + tag, bufs=1, align_bytes=64)
             nc.vector.quantize_mx(
                 out=codes[:].rearrange("p a n -> p (a n)").bitcast(FP8X4),
                 scales=scales[:].rearrange("p a n -> p (a n)"),
@@ -177,10 +181,10 @@ def tile_multiattention_pa_kernel(tc, attn_r, attn_d, v_d, out_rd, out_d):
         def av(h):
             s = st[h]
             codes, scales = s["ca"]
-            c0 = HD * (h % VG)
+            c0 = HD * (h % NHB)
             ob = ps.tile([P, 2, T, HD], F32, name="ob", tag="tw", bufs=3)
             for o in range(2):
-                vc, vs = st["v%d%d" % (o, h // VG)]
+                vc, vs = st["v%d%d" % (o, h // NHB)]
                 for i in range(T):
                     nc.tensor.matmul_mx(out=ob[:, o, i, :], lhsT=codes[:, o, P * i:P * i + P].bitcast(FP8X4),
                                         lhsT_scale=scales[:, o, P * i:P * i + P],
@@ -205,20 +209,18 @@ def tile_multiattention_pa_kernel(tc, attn_r, attn_d, v_d, out_rd, out_d):
                     nc.sync.dma_start(out=dst[b].rearrange("(i p) c -> p i c", p=P)[:, :, c0:c0 + w],
                                       in_=ot[:, o, :, HD * q0:HD * q0 + w])
 
-        def vgroup(v):
-            for o in range(2):
-                grp = sb.tile([P, VG, HD, 4], BF16, name="vgrp", tag="vgrp", bufs=4, align_bytes=64)
-                nc.gpsimd.tensor_scalar(out=grp[:], in0=vraw[o][:, VG * v:VG * v + VG].rearrange("p g j d -> p g d j"),
-                                        scalar1=1.0, scalar2=0.0, op0=ALU.mult, op1=ALU.add)
-                st["vg%d%d" % (o, v)] = grp
+        def vgroup(b, o):
+            grp = sb.tile([P, NHB, HD, 4], BF16, name="vg%d" % o, tag="vg%d" % o, bufs=1, align_bytes=64)
+            nc.gpsimd.tensor_scalar(out=grp[:], in0=vraw[o][:, NHB * b:NHB * b + NHB].rearrange("p g j d -> p g d j"),
+                                    scalar1=1.0, scalar2=0.0, op0=ALU.mult, op1=ALU.add)
+            st["vg%d%d" % (o, b)] = grp
 
-        def q_v(v):
-            for o in range(2):
-                codes = sb.tile([P, VG * HD], U32, name="cv", tag="cv", bufs=4, align_bytes=64)
-                scales = sb.tile([P, VG * HD], U8, name="sv", tag="sv", bufs=4, align_bytes=64)
-                nc.vector.quantize_mx(out=codes[:].bitcast(FP8X4), scales=scales[:],
-                                      in_=st["vg%d%d" % (o, v)][:].rearrange("p g d j -> p (g d j)"))
-                st["v%d%d" % (o, v)] = (codes, scales)
+        def q_v(b, o):
+            codes = sb.tile([P, NHB * HD], U32, name="cv%d" % o, tag="cv%d" % o, bufs=2, align_bytes=64)
+            scales = sb.tile([P, NHB * HD], U8, name="sv%d" % o, tag="sv%d" % o, bufs=2, align_bytes=64)
+            nc.vector.quantize_mx(out=codes[:].bitcast(FP8X4), scales=scales[:],
+                                  in_=st["vg%d%d" % (o, b)][:].rearrange("p g d j -> p (g d j)"))
+            st["v%d%d" % (o, b)] = (codes, scales)
 
         zero = const.tile([P, 8], F32, name="warm")
         nc.vector.memset(zero[:], 0.0)
@@ -259,39 +261,43 @@ def tile_multiattention_pa_kernel(tc, attn_r, attn_d, v_d, out_rd, out_d):
             if on(cur):
                 for i in range(T):
                     pmul(cur, i)
-            if on(old):
-                if old % VG == 0:
-                    q_v(old // VG)
-                q_a(old)
-            late = []
             more = []
             if it < 0:
                 if on(scl):
                     recip(scl)
                     root(scl)
+                    gate(scl)
                     for m, t in tiles:
                         wk(scl, m, t)
                 for m, t in tiles:
                     rows(new, m, t, new < 2 and t % 2 == 1)
             else:
-                if on(new):
-                    for m, t in tiles[:4]:
-                        rows(new, m, t, False)
-                    more = tiles[4:]
                 if on(scl):
                     recip(scl)
+                if on(new):
+                    for m, t in tiles[:2]:
+                        rows(new, m, t, False)
+                    more = tiles[2:]
+                if on(scl):
                     root(scl)
+            if on(old):
+                if old % NHB == 0:
+                    for o in range(2):
+                        q_v(old // NHB, o)
+                q_a(old)
+            if on(scl) and it >= 0:
+                for e in ("v", "g"):
+                    if e == "g":
+                        gate(scl)
                     for m, t in tiles:
-                        if wk_engine(scl, m, t) == "s":
-                            late.append((m, t))
-                        else:
+                        if wk_engine(scl, m, t) == e:
                             wk(scl, m, t)
+            for m, t in more[:3]:
+                rows(new, m, t, False)
             if on(old):
                 av(old)
             if on(nxt):
                 cols(nxt, 0)
-            if more:
-                rows(new, *more.pop(0), False)
             if on(old):
                 ocopy(old)
             if on(nxt):
@@ -299,18 +305,23 @@ def tile_multiattention_pa_kernel(tc, attn_r, attn_d, v_d, out_rd, out_d):
                     turn(nxt, 1, b2)
                     turn_copy(nxt, 1, b2)
                 dbc(nxt, 1)
-            if more:
-                rows(new, *more.pop(0), False)
+            for m, t in more[3:4]:
+                rows(new, m, t, False)
             if on(cur):
                 for i in range(T):
                     amix(cur, i)
                     aturn(cur, i)
                     acopy(cur, i)
-            for m, t in more:
+            for m, t in more[4:]:
                 rows(new, m, t, False)
-            for m, t in late:
-                wk(scl, m, t)
+            if on(scl) and it >= 0:
+                for m, t in tiles:
+                    if wk_engine(scl, m, t) == "s":
+                        wk(scl, m, t)
             if on(nxt):
                 cols(nxt, 1)
-                if nxt % VG == 0:
-                    vgroup(nxt // VG)
+            for o in range(2):
+                if it == -1:
+                    vgroup(0, o)
+                if it == NHB - 4 + o:
+                    vgroup(1, o)

@@ -23,7 +23,7 @@ BETA = 0.4
 FLOPS = NH * (2 * N * N * N + 2 * 2 * N * N * HD)
 
 WK_SCALAR = ((1, 3),)
-WK_VECTOR = ((0, 0), (1, 0))
+WK_VECTOR = ()
 PLAIN = 7
 
 
@@ -41,11 +41,10 @@ def tile_multiattention_pa_kernel(tc, attn_r, attn_d, v_d, out_rd, out_d):
         def load(h, pieces):
             s = {}
             st[h] = s
+            w = T // pieces
             for m in range(2):
                 s["n%d" % m] = sb.tile([P, T, N], BF16, name="n%d" % m, tag="n%d" % m, bufs=5 + m)
-            w = T // pieces
-            for c in range(pieces):
-                for m in range(2):
+                for c in range(pieces):
                     nc.sync.dma_start(out=s["n%d" % m][:, w * c:w * c + w, :], in_=maps[m][h][:, w * c:w * c + w, :])
 
         def rows(h, m, t, vector):
@@ -54,32 +53,36 @@ def tile_multiattention_pa_kernel(tc, attn_r, attn_d, v_d, out_rd, out_d):
                 s["x0"] = sb.tile([P, T, N], F32, name="x0", tag="x0", bufs=4)
                 s["x1"] = sb.tile([P, T, N], F32, name="x1", tag="x1", bufs=4)
                 s["rs"] = sb.tile([P, 2 * T], F32, name="rs", tag="rs", bufs=3)
-            src = s["n%d" % m][:, t, :]
-            dst = s["x%d" % m][:, t, :]
+            src = s["n%d" % m][:, t, :].rearrange("p (u q e) -> p u e q", u=2, e=2)
+            dst = s["x%d" % m][:, t, :].rearrange("p (u e q) -> p u e q", u=2, e=2)
             acc = s["rs"][:, T * m + t:T * m + t + 1]
             if vector:
                 nc.vector.tensor_scalar(out=dst, in0=src, scalar1=BETA, scalar2=0.0, op0=ALU.mult, op1=ALU.add, accum_out=acc)
             else:
                 nc.scalar.activation(out=dst, in_=src, func=ACT.Copy, scale=BETA, accum_out=acc)
 
-        def recip(h):
+        def recip(h, m0=0, m1=2):
             s = st[h]
-            s["inv"] = sb.tile([P, 2 * T], F32, name="inv", tag="inv")
-            nc.vector.reciprocal(out=s["inv"][:], in_=s["rs"][:])
+            if m0 == 0:
+                s["inv"] = sb.tile([P, 2 * T], F32, name="inv", tag="inv")
+            nc.vector.reciprocal(out=s["inv"][:, T * m0:T * m1], in_=s["rs"][:, T * m0:T * m1])
 
         def gate(h):
             s = st[h]
             s["zero"] = sb.tile([P, 2 * T], F32, name="zero", tag="zero")
             nc.vector.memset(s["zero"][:], 0.0)
 
-        def root(h):
+        def root(h, m0=0, m1=2):
             s = st[h]
-            s["d"] = sb.tile([P, 2 * T], F32, name="d", tag="d", bufs=3)
-            nc.scalar.activation(out=s["d"][:], in_=s["inv"][:], func=ACT.Sqrt, scale=BETA)
+            if m0 == 0:
+                s["d"] = sb.tile([P, 2 * T], F32, name="d", tag="d", bufs=3)
+            nc.scalar.activation(out=s["d"][:, T * m0:T * m1], in_=s["inv"][:, T * m0:T * m1], func=ACT.Sqrt, scale=BETA)
 
         def wk_engine(h, m, t):
             if h == 0:
-                return "s" if t == T - 1 else "v"
+                return "s" if m == 1 and t >= 2 else "v"
+            if h == 1:
+                return "s" if (m, t) == (1, T - 1) else "v"
             if (m, t) in WK_VECTOR:
                 return "v"
             return "s" if (m, t) in WK_SCALAR else "g"
@@ -90,6 +93,9 @@ def tile_multiattention_pa_kernel(tc, attn_r, attn_d, v_d, out_rd, out_d):
                 s["wk"] = [sb.tile([P, T, N], F32, name="wk%d" % i, tag="wk%d" % i, bufs=2) for i in range(2)]
             src = s["n%d" % m][:, t, :]
             dst = s["wk"][m][:, t, :]
+            if m == 1:
+                src = src.rearrange("p (u q e) -> p u e q", u=2, e=2)
+                dst = dst.rearrange("p (u e q) -> p u e q", u=2, e=2)
             col = s["d"][:, T * m + t:T * m + t + 1]
             e = wk_engine(h, m, t)
             if e == "g":
@@ -101,14 +107,21 @@ def tile_multiattention_pa_kernel(tc, attn_r, attn_d, v_d, out_rd, out_d):
 
         def dbc(h, m):
             s = st[h]
-            db = ps.tile([P, N], F32, name="dbc", tag="dbc", bufs=1)
+            if h == 0:
+                db = ps.tile([P, N], F32, name="dbc0", tag="pp", bufs=4)
+            else:
+                db = ps.tile([P, N], F32, name="dbc", tag="dbc", bufs=1)
             for c in range(T):
                 col = s["d"][:, T * m + c:T * m + c + 1].to_broadcast([P, P])
-                if h > 0 and T * m + c < PLAIN:
-                    nc.tensor.matmul(out=db[:, P * c:P * c + P], lhsT=col, rhs=ident[:], start=True, stop=True)
+                if m == 0:
+                    out, eye = db[:, P * c:P * c + P], ident[:]
                 else:
-                    nc.tensor.transpose(db[:, P * c:P * c + P], col, ident[:])
-            s["dbc"] = db
+                    half = db[:].rearrange("p (u e q) -> p u e q", u=2, e=2)
+                    out = half[:, c // 2, :, 64 * (c % 2):64 * (c % 2) + 64]
+                    eye = ident[:].rearrange("k (q e) -> k e q", e=2)
+                plain = h > 0 and T * m + c < PLAIN
+                nc.tensor.matmul(out=out, lhsT=col, rhs=eye, is_transpose=not plain, start=True, stop=True)
+            s["dbc%d" % m] = db
 
         def cols(h, m):
             s = st[h]
@@ -117,31 +130,34 @@ def tile_multiattention_pa_kernel(tc, attn_r, attn_d, v_d, out_rd, out_d):
             nc.vector.tensor_tensor(
                 out=s["gs"][:, m].rearrange("p (c i) t -> p c t i", i=4),
                 in0=s["wk"][m][:].rearrange("p t (c i) -> p c t i", i=4),
-                in1=s["dbc"][:].rearrange("p (c i) -> p c i", i=4).unsqueeze(2).to_broadcast([P, N // 4, 4, 4]),
+                in1=s["dbc%d" % m][:].rearrange("p (c i) -> p c i", i=4).unsqueeze(2).to_broadcast([P, N // 4, 4, 4]),
                 op=ALU.mult)
 
-        def quantise(src, tag):
-            codes = sb.tile([P, 2, N], U32, name="c" + tag, tag="c" + tag, bufs=1, align_bytes=64)
-            scales = sb.tile([P, 2, N], U8, name="s" + tag, tag="s" + tag, bufs=1, align_bytes=64)
+        def quantise(h, src, tag, n0, n1):
+            s = st[h]
+            if n0 == 0:
+                codes = sb.tile([P, 2 * N], U32, name="c" + tag, tag="c" + tag, bufs=2, align_bytes=64)
+                scales = sb.tile([P, 2 * N], U8, name="s" + tag, tag="s" + tag, bufs=2, align_bytes=64)
+                s["c" + tag] = (codes, scales)
+            codes, scales = s["c" + tag]
             nc.vector.quantize_mx(
-                out=codes[:].rearrange("p a n -> p (a n)").bitcast(FP8X4),
-                scales=scales[:].rearrange("p a n -> p (a n)"),
-                in_=src[:].rearrange("p a n t -> p (a n t)"))
-            return codes, scales
+                out=codes[:, n0:n1].bitcast(FP8X4),
+                scales=scales[:, n0:n1],
+                in_=src[:].rearrange("p a n t -> p (a n t)")[:, 4 * n0:4 * n1])
 
         def q_s(h):
-            st[h]["cs"] = quantise(st[h]["gs"], "s")
+            quantise(h, st[h]["gs"], "s", 0, 2 * N)
 
-        def q_a(h):
-            st[h]["ca"] = quantise(st[h]["gaw"], "a")
+        def q_a(h, n0=0, n1=2 * N):
+            quantise(h, st[h]["gaw"], "a", n0, n1)
 
         def pmul(h, i):
             s = st[h]
             codes, scales = s["cs"]
             pp = ps.tile([P, N], F32, name="pp", tag="pp", bufs=4)
-            nc.tensor.matmul_mx(out=pp[:], lhsT=codes[:, 0, P * i:P * i + P].bitcast(FP8X4),
-                                lhsT_scale=scales[:, 0, P * i:P * i + P],
-                                rhs=codes[:, 1, :].bitcast(FP8X4), rhs_scale=scales[:, 1, :], start=True, stop=True)
+            nc.tensor.matmul_mx(out=pp[:], lhsT=codes[:, P * i:P * i + P].bitcast(FP8X4),
+                                lhsT_scale=scales[:, P * i:P * i + P],
+                                rhs=codes[:, N:].bitcast(FP8X4), rhs_scale=scales[:, N:], start=True, stop=True)
             s["pp%d" % i] = pp
 
         def amix(h, i):
@@ -151,7 +167,7 @@ def tile_multiattention_pa_kernel(tc, attn_r, attn_d, v_d, out_rd, out_d):
 
         def aturn(h, i):
             s = st[h]
-            at = ps.tile([P, T, P], F32, name="at", tag="tw", bufs=3)
+            at = ps.tile([P, T, P], F32, name="at", tag="pp", bufs=4)
             for j in range(T):
                 for m in range(2):
                     nc.tensor.matmul(out=at[:, j, :], lhsT=s["x%d" % m][:, i, P * j:P * j + P], rhs=ident[:],
@@ -160,9 +176,9 @@ def tile_multiattention_pa_kernel(tc, attn_r, attn_d, v_d, out_rd, out_d):
 
         def acopy(h, i):
             s = st[h]
-            nc.scalar.copy(out=s["gaw"][:, 0, P * i:P * i + P, :], in_=s["at%d" % i][:].rearrange("p j n -> p n j"))
+            nc.scalar.copy(out=s["gaw"][:, 1, P * i:P * i + P, :], in_=s["at%d" % i][:].rearrange("p j n -> p n j"))
 
-        def turn(h, o, b2):
+        def turn(h, b2):
             s = st[h]
             if b2 == 0:
                 s["gaw"] = sb.tile([P, 2, N, 4], BF16, name="gaw", tag="gaw", bufs=2, align_bytes=64)
@@ -171,56 +187,60 @@ def tile_multiattention_pa_kernel(tc, attn_r, attn_d, v_d, out_rd, out_d):
             for ii in range(2):
                 for u in range(2):
                     nc.tensor.transpose(tw[:, u, P * ii:P * ii + P], words[:, 2 * b2 + ii, P * u:P * u + P], ident[:])
-            s["tw%d%d" % (o, b2)] = tw
+            s["tw%d" % b2] = tw
 
-        def turn_copy(h, o, b2):
+        def turn_copy(h, b2):
             s = st[h]
-            g32 = s["gaw"][:, o].bitcast(F32)
-            nc.scalar.copy(out=g32[:, 256 * b2:256 * b2 + 256, :], in_=s["tw%d%d" % (o, b2)][:].rearrange("p u n -> p n u"))
+            g32 = s["gaw"][:, 0].bitcast(F32)
+            nc.scalar.copy(out=g32[:, 256 * b2:256 * b2 + 256, :], in_=s["tw%d" % b2][:].rearrange("p u n -> p n u"))
 
-        def av(h):
+        def av(h, b0=0, b1=2 * T):
             s = st[h]
             codes, scales = s["ca"]
             c0 = HD * (h % NHB)
-            ob = ps.tile([P, 2, T, HD], F32, name="ob", tag="tw", bufs=3)
-            for o in range(2):
-                vc, vs = st["v%d%d" % (o, h // NHB)]
-                for i in range(T):
-                    nc.tensor.matmul_mx(out=ob[:, o, i, :], lhsT=codes[:, o, P * i:P * i + P].bitcast(FP8X4),
-                                        lhsT_scale=scales[:, o, P * i:P * i + P],
-                                        rhs=vc[:, c0:c0 + HD].bitcast(FP8X4), rhs_scale=vs[:, c0:c0 + HD],
-                                        start=True, stop=True)
-            s["ob"] = ob
+            vc, vs = st["v%d" % (h // NHB)]
+            if b0 == 0:
+                s["ob"] = ps.tile([P, 2 * T, HD], F32, name="ob", tag="tw", bufs=3)
+            for i in range(b0, b1):
+                nc.tensor.matmul_mx(out=s["ob"][:, i, :], lhsT=codes[:, P * i:P * i + P].bitcast(FP8X4),
+                                    lhsT_scale=scales[:, P * i:P * i + P],
+                                    rhs=vc[:, c0:c0 + HD].bitcast(FP8X4), rhs_scale=vs[:, c0:c0 + HD],
+                                    start=True, stop=True)
 
-        def ocopy(h):
+        def ocopy(h, b0=0, b1=2 * T):
             b = h // NHB
             k = h % NHB
             q = k % 2
-            if q == 0:
-                st["o"] = sb.tile([P, 2, T, 2 * HD], F32, name="o", tag="o", bufs=3)
+            if q == 0 and b0 == 0:
+                st["o"] = sb.tile([P, 2 * T, 2 * HD], F32, name="o", tag="o", bufs=3)
             ot = st["o"]
-            nc.scalar.copy(out=ot[:, :, :, HD * q:HD * q + HD], in_=st[h]["ob"][:])
+            nc.scalar.copy(out=ot[:, b0:b1, HD * q:HD * q + HD], in_=st[h]["ob"][:, b0:b1, :])
             last = h >= NH - 2
             if last or q == 1:
                 q0 = q if last else 0
                 c0 = HD * (k - q + q0)
                 w = HD * (q + 1 - q0)
-                for o, dst in enumerate((out_rd, out_d)):
-                    nc.sync.dma_start(out=dst[b].rearrange("(i p) c -> p i c", p=P)[:, :, c0:c0 + w],
-                                      in_=ot[:, o, :, HD * q0:HD * q0 + w])
+                for o, dst in enumerate((out_d, out_rd)):
+                    i0, i1 = max(b0, T * o), min(b1, T * o + T)
+                    if i0 < i1:
+                        nc.sync.dma_start(out=dst[b].rearrange("(i p) c -> p i c", p=P)[:, i0 - T * o:i1 - T * o, c0:c0 + w],
+                                          in_=ot[:, i0:i1, HD * q0:HD * q0 + w])
 
-        def vgroup(b, o):
-            grp = sb.tile([P, NHB, HD, 4], BF16, name="vg%d" % o, tag="vg%d" % o, bufs=1, align_bytes=64)
-            nc.gpsimd.tensor_scalar(out=grp[:], in0=vraw[o][:, NHB * b:NHB * b + NHB].rearrange("p g j d -> p g d j"),
-                                    scalar1=1.0, scalar2=0.0, op0=ALU.mult, op1=ALU.add)
-            st["vg%d%d" % (o, b)] = grp
+        def vgroup(b):
+            grp = sb.tile([P, NHB, HD, 4], BF16, name="vg", tag="vg", bufs=1, align_bytes=64)
+            src = vraw[:, NHB * b:NHB * b + NHB].rearrange("p g j d -> p g d j")
+            if b == 0:
+                nc.vector.tensor_copy(out=grp[:], in_=src)
+            else:
+                nc.gpsimd.tensor_scalar(out=grp[:], in0=src, scalar1=1.0, scalar2=0.0, op0=ALU.mult, op1=ALU.add)
+            st["vg%d" % b] = grp
 
-        def q_v(b, o):
-            codes = sb.tile([P, NHB * HD], U32, name="cv%d" % o, tag="cv%d" % o, bufs=2, align_bytes=64)
-            scales = sb.tile([P, NHB * HD], U8, name="sv%d" % o, tag="sv%d" % o, bufs=2, align_bytes=64)
+        def q_v(b):
+            codes = sb.tile([P, NHB * HD], U32, name="cv", tag="cv", bufs=2, align_bytes=64)
+            scales = sb.tile([P, NHB * HD], U8, name="sv", tag="sv", bufs=2, align_bytes=64)
             nc.vector.quantize_mx(out=codes[:].bitcast(FP8X4), scales=scales[:],
-                                  in_=st["vg%d%d" % (o, b)][:].rearrange("p g d j -> p (g d j)"))
-            st["v%d%d" % (o, b)] = (codes, scales)
+                                  in_=st["vg%d" % b][:].rearrange("p g d j -> p (g d j)"))
+            st["v%d" % b] = (codes, scales)
 
         zero = const.tile([P, 8], F32, name="warm")
         nc.vector.memset(zero[:], 0.0)
@@ -231,18 +251,42 @@ def tile_multiattention_pa_kernel(tc, attn_r, attn_d, v_d, out_rd, out_d):
         make_identity(nc, ident[:])
         load(1, 1)
         load(2, 1)
-        vraw = []
-        for o in range(2):
-            raw = const.tile([P, NH, 4, HD], BF16, name="vraw%d" % o)
-            vraw.append(raw)
-        nc.sync.dma_start(out=vraw[0][:].rearrange("p g j d -> p (g j) d"),
-                          in_=v_d.rearrange("b h (j p) d -> p (b h j) d", p=P))
-        nc.sync.dma_start(out=vraw[1][:].rearrange("p g (u e) d -> p (g u) (e d)", u=2),
+        vraw = const.tile([P, NH, 4, HD], BF16, name="vraw")
+        nc.sync.dma_start(out=vraw[:].rearrange("p g (u e) d -> p (g u) (e d)", u=2),
                           in_=v_d.rearrange("b h (u p e) d -> p (b h u) (e d)", u=2, e=2))
         load(3, 1)
 
         tiles = [(m, t) for m in range(2) for t in range(T)]
-        for it in range(-3, NH + 1):
+
+        def wk_on(h, e, maps=(0, 1)):
+            for m, t in tiles:
+                if m in maps and wk_engine(h, m, t) == e:
+                    wk(h, m, t)
+
+        def head_rows(h, part):
+            for m, t in part:
+                rows(h, m, t, False)
+
+        for t in range(T):
+            rows(0, 0, t, t % 2 == 1)
+        head_rows(0, ((1, 0), (1, 1)))
+        recip(0, 0, 1)
+        root(0, 0, 1)
+        dbc(0, 0)
+        wk_on(0, "v", (0,))
+        head_rows(0, ((1, 2), (1, 3)))
+        head_rows(1, tiles[:1])
+        recip(0, 1, 2)
+        root(0, 1, 2)
+        dbc(0, 1)
+        cols(0, 0)
+        wk_on(0, "v", (1,))
+        wk_on(0, "s", (1,))
+        head_rows(1, tiles[1:])
+        for b2 in range(2):
+            turn(0, b2)
+        cols(0, 1)
+        for it in range(NH):
             new = it + 3
             scl = it + 2
             nxt = it + 1
@@ -252,76 +296,71 @@ def tile_multiattention_pa_kernel(tc, attn_r, attn_d, v_d, out_rd, out_d):
             def on(h):
                 return 0 <= h < NH
 
-            if on(it + 4) and it + 4 > 3:
+            if on(it + 4):
                 load(it + 4, 1)
-            if on(cur):
-                q_s(cur)
+            if on(scl) and it > 0:
+                recip(scl)
+                root(scl)
+            q_s(cur)
+            if it == 0:
+                recip(1)
+                head_rows(2, tiles[:1])
+                root(1)
+                wk_on(1, "v")
+                wk_on(1, "s")
+                vgroup(0)
+                head_rows(2, tiles[1:])
+                for b2 in range(2):
+                    turn_copy(0, b2)
             if on(nxt):
                 dbc(nxt, 0)
-            if on(cur):
-                for i in range(T):
-                    pmul(cur, i)
-            more = []
-            if it < 0:
-                if on(scl):
-                    recip(scl)
-                    root(scl)
-                    gate(scl)
-                    for m, t in tiles:
-                        wk(scl, m, t)
-                for m, t in tiles:
-                    rows(new, m, t, new < 2 and t % 2 == 1)
-            else:
-                if on(scl):
-                    recip(scl)
-                if on(new):
-                    for m, t in tiles[:2]:
-                        rows(new, m, t, False)
-                    more = tiles[2:]
-                if on(scl):
-                    root(scl)
+            for i in range(T):
+                pmul(cur, i)
             if on(old):
                 if old % NHB == 0:
-                    for o in range(2):
-                        q_v(old // NHB, o)
+                    q_v(old // NHB)
                 q_a(old)
-            if on(scl) and it >= 0:
-                for e in ("v", "g"):
-                    if e == "g":
-                        gate(scl)
-                    for m, t in tiles:
-                        if wk_engine(scl, m, t) == e:
-                            wk(scl, m, t)
-            for m, t in more[:3]:
-                rows(new, m, t, False)
+            if on(scl) and it > 0:
+                wk_on(scl, "v")
+                gate(scl)
+                wk_on(scl, "g")
+            if it == 0:
+                cols(1, 0)
+                recip(2)
+                root(2)
+                gate(2)
+                wk_on(2, "g")
+            if on(new):
+                head_rows(new, tiles[:5])
             if on(old):
                 av(old)
-            if on(nxt):
+            if on(nxt) and it > 0:
                 cols(nxt, 0)
             if on(old):
                 ocopy(old)
             if on(nxt):
                 for b2 in range(2):
-                    turn(nxt, 1, b2)
-                    turn_copy(nxt, 1, b2)
+                    turn(nxt, b2)
+                    turn_copy(nxt, b2)
                 dbc(nxt, 1)
-            for m, t in more[3:4]:
-                rows(new, m, t, False)
-            if on(cur):
-                for i in range(T):
-                    amix(cur, i)
-                    aturn(cur, i)
-                    acopy(cur, i)
-            for m, t in more[4:]:
-                rows(new, m, t, False)
-            if on(scl) and it >= 0:
-                for m, t in tiles:
-                    if wk_engine(scl, m, t) == "s":
-                        wk(scl, m, t)
+            if on(new):
+                head_rows(new, tiles[5:])
+            if on(scl):
+                wk_on(scl, "s")
+            if nxt == NH:
+                q_a(cur, 0, N)
+            for i in range(T):
+                amix(cur, i)
+                aturn(cur, i)
+                acopy(cur, i)
+            if nxt == NH:
+                av(cur, 0, T)
+                ocopy(cur, 0, T)
+                for i in range(T, 2 * T, 2):
+                    q_a(cur, P * i, P * i + 2 * P)
+                    av(cur, i, i + 2)
+                    ocopy(cur, i, i + 2)
             if on(nxt):
                 cols(nxt, 1)
-            for o in range(2):
-                if it == -1:
-                    vgroup(0, o)
-                if it == NHB - 4 + o:
-                    vgroup(1, o)
+            if it == NHB // 2:
+                vgroup(1)

@@ -50,8 +50,8 @@ def tile_multiattention_pa_kernel(tc, attn_r, attn_d, v_d, out_rd, out_d):
         def rows(h, m, t, vector):
             s = st[h]
             if m == 0 and t == 0:
-                s["x0"] = sb.tile([P, T, N], F32, name="x0", tag="x0", bufs=4)
-                s["x1"] = sb.tile([P, T, N], F32, name="x1", tag="x1", bufs=4)
+                s["x0"] = sb.tile([P, T, N], F32, name="x0", tag="x0", bufs=3)
+                s["x1"] = sb.tile([P, T, N], F32, name="x1", tag="x1", bufs=3)
                 s["rs"] = sb.tile([P, 2 * T], F32, name="rs", tag="rs", bufs=3)
             src = s["n%d" % m][:, t, :].rearrange("p (u q e) -> p u e q", u=2, e=2)
             dst = s["x%d" % m][:, t, :].rearrange("p (u e q) -> p u e q", u=2, e=2)
@@ -81,8 +81,6 @@ def tile_multiattention_pa_kernel(tc, attn_r, attn_d, v_d, out_rd, out_d):
         def wk_engine(h, m, t):
             if h == 0:
                 return "s" if m == 1 and t >= 2 else "v"
-            if h == 1:
-                return "s" if (m, t) == (1, T - 1) else "v"
             if (m, t) in WK_VECTOR:
                 return "v"
             return "s" if (m, t) in WK_SCALAR else "g"
@@ -119,7 +117,7 @@ def tile_multiattention_pa_kernel(tc, attn_r, attn_d, v_d, out_rd, out_d):
                     half = db[:].rearrange("p (u e q) -> p u e q", u=2, e=2)
                     out = half[:, c // 2, :, 64 * (c % 2):64 * (c % 2) + 64]
                     eye = ident[:].rearrange("k (q e) -> k e q", e=2)
-                plain = h > 0 and T * m + c < PLAIN
+                plain = h > 1 and T * m + c < PLAIN
                 nc.tensor.matmul(out=out, lhsT=col, rhs=eye, is_transpose=not plain, start=True, stop=True)
             s["dbc%d" % m] = db
 
@@ -154,18 +152,21 @@ def tile_multiattention_pa_kernel(tc, attn_r, attn_d, v_d, out_rd, out_d):
         def pmul(h, i):
             s = st[h]
             codes, scales = s["cs"]
-            pp = ps.tile([P, N], F32, name="pp", tag="pp", bufs=4)
-            nc.tensor.matmul_mx(out=pp[:], lhsT=codes[:, P * i:P * i + P].bitcast(FP8X4),
-                                lhsT_scale=scales[:, P * i:P * i + P],
-                                rhs=codes[:, N:].bitcast(FP8X4), rhs_scale=scales[:, N:], start=True, stop=True)
+            pp = ps.tile([P, T, P], F32, name="pp", tag="pp", bufs=4)
+            for j in range(T):
+                d0 = N + P * j
+                nc.tensor.matmul_mx(out=pp[:, j, :], lhsT=codes[:, d0:d0 + P].bitcast(FP8X4), lhsT_scale=scales[:, d0:d0 + P],
+                                    rhs=codes[:, P * i:P * i + P].bitcast(FP8X4), rhs_scale=scales[:, P * i:P * i + P],
+                                    start=True, stop=True)
             s["pp%d" % i] = pp
 
         def amix(h, i):
             s = st[h]
-            nc.vector.scalar_tensor_tensor(out=s["x0"][:, i, :], in0=s["pp%d" % i][:], scalar=ALPHA,
-                                           in1=s["x0"][:, i, :], op0=ALU.mult, op1=ALU.add)
+            nc.vector.scalar_tensor_tensor(out=s["gaw"][:, 1, P * i:P * i + P, :],
+                                           in0=s["pp%d" % i][:].rearrange("p j n -> p n j"), scalar=ALPHA,
+                                           in1=s["xt"][:, P * i:P * i + P, :], op0=ALU.mult, op1=ALU.add)
 
-        def aturn(h, i):
+        def xturn(h, i):
             s = st[h]
             at = ps.tile([P, T, P], F32, name="at", tag="pp", bufs=4)
             for j in range(T):
@@ -174,9 +175,15 @@ def tile_multiattention_pa_kernel(tc, attn_r, attn_d, v_d, out_rd, out_d):
                                      is_transpose=True, start=m == 0, stop=m == 1)
             s["at%d" % i] = at
 
-        def acopy(h, i):
+        def xcopy(h, i):
             s = st[h]
-            nc.scalar.copy(out=s["gaw"][:, 1, P * i:P * i + P, :], in_=s["at%d" % i][:].rearrange("p j n -> p n j"))
+            if i == 0:
+                s["xt"] = sb.tile([P, N, T], F32, name="xt", tag="xt", bufs=3)
+            out, in_ = s["xt"][:, P * i:P * i + P, :], s["at%d" % i][:].rearrange("p j n -> p n j")
+            if h == 0:
+                nc.vector.tensor_copy(out=out, in_=in_)
+            else:
+                nc.scalar.copy(out=out, in_=in_)
 
         def turn(h, b2):
             s = st[h]
@@ -229,10 +236,7 @@ def tile_multiattention_pa_kernel(tc, attn_r, attn_d, v_d, out_rd, out_d):
         def vgroup(b):
             grp = sb.tile([P, NHB, HD, 4], BF16, name="vg", tag="vg", bufs=1, align_bytes=64)
             src = vraw[:, NHB * b:NHB * b + NHB].rearrange("p g j d -> p g d j")
-            if b == 0:
-                nc.vector.tensor_copy(out=grp[:], in_=src)
-            else:
-                nc.gpsimd.tensor_scalar(out=grp[:], in0=src, scalar1=1.0, scalar2=0.0, op0=ALU.mult, op1=ALU.add)
+            nc.vector.tensor_copy(out=grp[:], in_=src)
             st["vg%d" % b] = grp
 
         def q_v(b):
@@ -290,55 +294,59 @@ def tile_multiattention_pa_kernel(tc, attn_r, attn_d, v_d, out_rd, out_d):
             new = it + 3
             scl = it + 2
             nxt = it + 1
-            cur = it
-            old = it - 1
 
             def on(h):
-                return 0 <= h < NH
+                return h < NH
 
             if on(it + 4):
                 load(it + 4, 1)
             if on(scl) and it > 0:
                 recip(scl)
                 root(scl)
-            q_s(cur)
+            if it > 0:
+                q_a(it - 1)
+            q_s(it)
             if it == 0:
                 recip(1)
-                head_rows(2, tiles[:1])
-                root(1)
-                wk_on(1, "v")
-                wk_on(1, "s")
-                vgroup(0)
-                head_rows(2, tiles[1:])
+                gate(1)
                 for b2 in range(2):
                     turn_copy(0, b2)
+                root(1)
+                wk_on(1, "g")
+                for i in range(T):
+                    xturn(0, i)
+                    xcopy(0, i)
+                wk_on(1, "s")
+                head_rows(2, tiles)
+                vgroup(0)
             if on(nxt):
                 dbc(nxt, 0)
+            if it > 0:
+                if (it - 1) % NHB == 0:
+                    q_v((it - 1) // NHB)
+                av(it - 1)
             for i in range(T):
-                pmul(cur, i)
-            if on(old):
-                if old % NHB == 0:
-                    q_v(old // NHB)
-                q_a(old)
+                pmul(it, i)
             if on(scl) and it > 0:
                 wk_on(scl, "v")
                 gate(scl)
                 wk_on(scl, "g")
             if it == 0:
+                for i in range(T):
+                    amix(0, i)
                 cols(1, 0)
                 recip(2)
-                root(2)
                 gate(2)
-                wk_on(2, "g")
             if on(new):
                 head_rows(new, tiles[:5])
-            if on(old):
-                av(old)
-            if on(nxt) and it > 0:
-                cols(nxt, 0)
-            if on(old):
-                ocopy(old)
+            if it == 0:
+                root(2)
+                wk_on(2, "g")
+            if it > 0:
+                ocopy(it - 1)
             if on(nxt):
+                if it > 0:
+                    cols(nxt, 0)
                 for b2 in range(2):
                     turn(nxt, b2)
                     turn_copy(nxt, b2)
@@ -348,19 +356,20 @@ def tile_multiattention_pa_kernel(tc, attn_r, attn_d, v_d, out_rd, out_d):
             if on(scl):
                 wk_on(scl, "s")
             if nxt == NH:
-                q_a(cur, 0, N)
+                q_a(it, 0, N)
+                av(it, 0, T)
             for i in range(T):
-                amix(cur, i)
-                aturn(cur, i)
-                acopy(cur, i)
-            if nxt == NH:
-                av(cur, 0, T)
-                ocopy(cur, 0, T)
-                for i in range(T, 2 * T, 2):
-                    q_a(cur, P * i, P * i + 2 * P)
-                    av(cur, i, i + 2)
-                    ocopy(cur, i, i + 2)
+                if it > 0:
+                    amix(it, i)
+                if on(nxt):
+                    xturn(nxt, i)
+                    xcopy(nxt, i)
             if on(nxt):
                 cols(nxt, 1)
             if it == NHB // 2:
                 vgroup(1)
+        ocopy(NH - 1, 0, T)
+        for i in range(T, 2 * T, 2):
+            q_a(NH - 1, P * i, P * i + 2 * P)
+            av(NH - 1, i, i + 2)
+            ocopy(NH - 1, i, i + 2)

@@ -126,9 +126,9 @@ def tile_multiattention_pa_kernel(tc, attn_r, attn_d, v_d, out_rd, out_d):
             if m == 0:
                 s["gs"] = sb.tile([P, 2, N, 4], BF16, name="gs", tag="gs", bufs=1, align_bytes=64)
             nc.vector.tensor_tensor(
-                out=s["gs"][:, m].rearrange("p (c i) t -> p c t i", i=4),
-                in0=s["wk"][m][:].rearrange("p t (c i) -> p c t i", i=4),
-                in1=s["dbc%d" % m][:].rearrange("p (c i) -> p c i", i=4).unsqueeze(2).to_broadcast([P, N // 4, 4, 4]),
+                out=s["gs"][:, m].rearrange("p (c i) t -> p c t i", i=2),
+                in0=s["wk"][m][:].rearrange("p t (c i) -> p c t i", i=2),
+                in1=s["dbc%d" % m][:].rearrange("p (c i) -> p c i", i=2).unsqueeze(2).to_broadcast([P, N // 2, 4, 2]),
                 op=ALU.mult)
 
         def quantise(h, src, tag, n0, n1):

@@ -22,8 +22,7 @@ BETA = 0.4
 
 FLOPS = NH * (2 * N * N * N + 2 * 2 * N * N * HD)
 
-WK_SCALAR = ((1, 3),)
-WK_VECTOR = ()
+BLOCK = (0, 2, 1, 3)
 PLAIN = 7
 
 
@@ -50,58 +49,28 @@ def tile_multiattention_pa_kernel(tc, attn_r, attn_d, v_d, out_rd, out_d):
         def rows(h, m, t, vector):
             s = st[h]
             if m == 0 and t == 0:
-                s["x0"] = sb.tile([P, T, N], F32, name="x0", tag="x0", bufs=3)
-                s["x1"] = sb.tile([P, T, N], F32, name="x1", tag="x1", bufs=3)
+                s["x0"] = sb.tile([P, T, N], F32, name="x0", tag="x0", bufs=4)
+                s["x1"] = sb.tile([P, T, N], F32, name="x1", tag="x1", bufs=4)
                 s["rs"] = sb.tile([P, 2 * T], F32, name="rs", tag="rs", bufs=3)
-            src = s["n%d" % m][:, t, :].rearrange("p (u q e) -> p u e q", u=2, e=2)
-            dst = s["x%d" % m][:, t, :].rearrange("p (u e q) -> p u e q", u=2, e=2)
+            src = s["n%d" % m][:, t, :].rearrange("p (r e) -> p e r", e=2)
+            dst = s["x%d" % m][:, t, :].rearrange("p (e r) -> p e r", e=2)
             acc = s["rs"][:, T * m + t:T * m + t + 1]
             if vector:
-                nc.vector.tensor_scalar(out=dst, in0=src, scalar1=BETA, scalar2=0.0, op0=ALU.mult, op1=ALU.add, accum_out=acc)
+                nc.vector.tensor_scalar(out=dst, in0=src, scalar1=1.0, scalar2=0.0, op0=ALU.mult, op1=ALU.add, accum_out=acc)
             else:
-                nc.scalar.activation(out=dst, in_=src, func=ACT.Copy, scale=BETA, accum_out=acc)
+                nc.scalar.activation(out=dst, in_=src, func=ACT.Copy, accum_out=acc)
 
-        def recip(h, m0=0, m1=2):
-            s = st[h]
-            if m0 == 0:
-                s["inv"] = sb.tile([P, 2 * T], F32, name="inv", tag="inv")
-            nc.vector.reciprocal(out=s["inv"][:, T * m0:T * m1], in_=s["rs"][:, T * m0:T * m1])
-
-        def gate(h):
-            s = st[h]
-            s["zero"] = sb.tile([P, 2 * T], F32, name="zero", tag="zero")
-            nc.vector.memset(s["zero"][:], 0.0)
-
-        def root(h, m0=0, m1=2):
+        def power(h, m0=0, m1=2):
             s = st[h]
             if m0 == 0:
                 s["d"] = sb.tile([P, 2 * T], F32, name="d", tag="d", bufs=3)
-            nc.scalar.activation(out=s["d"][:, T * m0:T * m1], in_=s["inv"][:, T * m0:T * m1], func=ACT.Sqrt, scale=BETA)
+            w = slice(T * m0, T * m1)
+            nc.gpsimd.tensor_tensor(out=s["d"][:, w], in0=s["rs"][:, w], in1=mhalf[:, w], op=ALU.pow)
 
-        def wk_engine(h, m, t):
-            if h == 0:
-                return "s" if m == 1 and t >= 2 else "v"
-            if (m, t) in WK_VECTOR:
-                return "v"
-            return "s" if (m, t) in WK_SCALAR else "g"
-
-        def wk(h, m, t):
+        def gate(h):
             s = st[h]
-            if "wk" not in s:
-                s["wk"] = [sb.tile([P, T, N], F32, name="wk%d" % i, tag="wk%d" % i, bufs=2) for i in range(2)]
-            src = s["n%d" % m][:, t, :]
-            dst = s["wk"][m][:, t, :]
-            if m == 1:
-                src = src.rearrange("p (u q e) -> p u e q", u=2, e=2)
-                dst = dst.rearrange("p (u e q) -> p u e q", u=2, e=2)
-            col = s["d"][:, T * m + t:T * m + t + 1]
-            e = wk_engine(h, m, t)
-            if e == "g":
-                nc.gpsimd.tensor_scalar(out=dst, in0=src, scalar1=col, scalar2=s["zero"][:, 0:1], op0=ALU.mult, op1=ALU.add)
-            elif e == "v":
-                nc.vector.tensor_scalar(out=dst, in0=src, scalar1=col, scalar2=None, op0=ALU.mult)
-            else:
-                nc.scalar.activation(out=dst, in_=src, func=ACT.Copy, scale=col)
+            s["zero"] = sb.tile([P, 2], F32, name="zero", tag="zero")
+            nc.vector.memset(s["zero"][:], 0.0)
 
         def dbc(h, m):
             s = st[h]
@@ -114,22 +83,36 @@ def tile_multiattention_pa_kernel(tc, attn_r, attn_d, v_d, out_rd, out_d):
                 if m == 0:
                     out, eye = db[:, P * c:P * c + P], ident[:]
                 else:
-                    half = db[:].rearrange("p (u e q) -> p u e q", u=2, e=2)
-                    out = half[:, c // 2, :, 64 * (c % 2):64 * (c % 2) + 64]
+                    out = db[:].rearrange("p (e r) -> p e r", e=2)[:, :, 64 * c:64 * c + 64]
                     eye = ident[:].rearrange("k (q e) -> k e q", e=2)
-                plain = h > 1 and T * m + c < PLAIN
+                plain = h > 2 and T * m + c < PLAIN
                 nc.tensor.matmul(out=out, lhsT=col, rhs=eye, is_transpose=not plain, start=True, stop=True)
             s["dbc%d" % m] = db
 
-        def cols(h, m):
+        def scale(h, m):
+            s = st[h]
+            s["sn%d" % m] = sb.tile([P, T, N], BF16, name="sn%d" % m, tag="sn%d" % m, bufs=2)
+            for t in range(T):
+                src = s["n%d" % m][:, t, :]
+                dst = s["sn%d" % m][:, t, :]
+                bc = s["dbc%d" % m][:]
+                if m == 1:
+                    src = src.rearrange("p (r e) -> p e r", e=2)
+                    dst = dst.rearrange("p (e r) -> p e r", e=2)
+                    bc = bc.rearrange("p (e r) -> p e r", e=2)
+                nc.vector.scalar_tensor_tensor(out=dst, in0=src, scalar=s["d"][:, T * m + t:T * m + t + 1],
+                                               in1=bc, op0=ALU.mult, op1=ALU.mult)
+
+        def lace(h, m, vector):
             s = st[h]
             if m == 0:
-                s["gs"] = sb.tile([P, 2, N, 4], BF16, name="gs", tag="gs", bufs=1, align_bytes=64)
-            nc.vector.tensor_tensor(
-                out=s["gs"][:, m].rearrange("p (c i) t -> p c t i", i=2),
-                in0=s["wk"][m][:].rearrange("p t (c i) -> p c t i", i=2),
-                in1=s["dbc%d" % m][:].rearrange("p (c i) -> p c i", i=2).unsqueeze(2).to_broadcast([P, N // 2, 4, 2]),
-                op=ALU.mult)
+                s["gs"] = sb.tile([P, 2, N, 4], BF16, name="gs", tag="gs", bufs=2, align_bytes=64)
+            src = s["sn%d" % m][:].rearrange("p t n -> p n t")
+            if vector:
+                nc.vector.tensor_copy(out=s["gs"][:, m], in_=src)
+            else:
+                add = s["zero"][:, 0:1] if m == 0 and "zero" in s else 0.0
+                nc.gpsimd.tensor_scalar(out=s["gs"][:, m], in0=src, scalar1=1.0, scalar2=add, op0=ALU.mult, op1=ALU.add)
 
         def quantise(h, src, tag, n0, n1):
             s = st[h]
@@ -154,7 +137,7 @@ def tile_multiattention_pa_kernel(tc, attn_r, attn_d, v_d, out_rd, out_d):
             codes, scales = s["cs"]
             pp = ps.tile([P, T, P], F32, name="pp", tag="pp", bufs=4)
             for j in range(T):
-                d0 = N + P * j
+                d0 = N + P * BLOCK[j]
                 nc.tensor.matmul_mx(out=pp[:, j, :], lhsT=codes[:, d0:d0 + P].bitcast(FP8X4), lhsT_scale=scales[:, d0:d0 + P],
                                     rhs=codes[:, P * i:P * i + P].bitcast(FP8X4), rhs_scale=scales[:, P * i:P * i + P],
                                     start=True, stop=True)
@@ -168,22 +151,19 @@ def tile_multiattention_pa_kernel(tc, attn_r, attn_d, v_d, out_rd, out_d):
 
         def xturn(h, i):
             s = st[h]
-            at = ps.tile([P, T, P], F32, name="at", tag="pp", bufs=4)
+            at = ps.tile([P, T, P], F32, name="at", tag="tw" if h == NH - 1 else "pp", bufs=3 if h == NH - 1 else 4)
             for j in range(T):
                 for m in range(2):
-                    nc.tensor.matmul(out=at[:, j, :], lhsT=s["x%d" % m][:, i, P * j:P * j + P], rhs=ident[:],
+                    nc.tensor.matmul(out=at[:, j, :], lhsT=s["x%d" % m][:, i, P * BLOCK[j]:P * BLOCK[j] + P], rhs=ident[:],
                                      is_transpose=True, start=m == 0, stop=m == 1)
             s["at%d" % i] = at
 
         def xcopy(h, i):
             s = st[h]
-            if i == 0:
+            if "xt" not in s:
                 s["xt"] = sb.tile([P, N, T], F32, name="xt", tag="xt", bufs=3)
             out, in_ = s["xt"][:, P * i:P * i + P, :], s["at%d" % i][:].rearrange("p j n -> p n j")
-            if h == 0:
-                nc.vector.tensor_copy(out=out, in_=in_)
-            else:
-                nc.scalar.copy(out=out, in_=in_)
+            nc.scalar.activation(out=out, in_=in_, func=ACT.Copy, scale=BETA)
 
         def turn(h, b2):
             s = st[h]
@@ -233,11 +213,12 @@ def tile_multiattention_pa_kernel(tc, attn_r, attn_d, v_d, out_rd, out_d):
                         nc.sync.dma_start(out=dst[b].rearrange("(i p) c -> p i c", p=P)[:, i0 - T * o:i1 - T * o, c0:c0 + w],
                                           in_=ot[:, i0:i1, HD * q0:HD * q0 + w])
 
-        def vgroup(b):
-            grp = sb.tile([P, NHB, HD, 4], BF16, name="vg", tag="vg", bufs=1, align_bytes=64)
-            src = vraw[:, NHB * b:NHB * b + NHB].rearrange("p g j d -> p g d j")
-            nc.vector.tensor_copy(out=grp[:], in_=src)
-            st["vg%d" % b] = grp
+        def vgroup(b, g0, g1):
+            if g0 == 0:
+                st["vg%d" % b] = sb.tile([P, NHB, HD, 4], BF16, name="vg", tag="vg", bufs=1, align_bytes=64)
+            src = vraw[:, NHB * b + g0:NHB * b + g1].rearrange("p g j d -> p g d j")
+            add = st[1]["zero"][:, 0:1] if b == 0 else 0.0
+            nc.gpsimd.tensor_scalar(out=st["vg%d" % b][:, g0:g1], in0=src, scalar1=1.0, scalar2=add, op0=ALU.mult, op1=ALU.add)
 
         def q_v(b):
             codes = sb.tile([P, NHB * HD], U32, name="cv", tag="cv", bufs=2, align_bytes=64)
@@ -246,128 +227,118 @@ def tile_multiattention_pa_kernel(tc, attn_r, attn_d, v_d, out_rd, out_d):
                                   in_=st["vg%d" % b][:].rearrange("p g d j -> p (g d j)"))
             st["v%d" % b] = (codes, scales)
 
-        zero = const.tile([P, 8], F32, name="warm")
-        nc.vector.memset(zero[:], 0.0)
-        warm = const.tile([P, 8], F32, name="warm_out")
-        nc.scalar.activation(out=warm[:], in_=zero[:], func=ACT.Sqrt)
+        mhalf = const.tile([P, 2 * T], F32, name="mhalf")
+        nc.gpsimd.memset(mhalf[:], -0.5)
         load(0, T)
         ident = const.tile([P, P], F32, name="ident")
         make_identity(nc, ident[:])
+        vraw = const.tile([P, NH, 4, HD], BF16, name="vraw")
+
+        def vload(b):
+            nc.sync.dma_start(out=vraw[:, NHB * b:NHB * b + NHB].rearrange("p g (u e) d -> p (g u) (e d)", u=2),
+                              in_=v_d[b].rearrange("h (u p e) d -> p (h u) (e d)", u=2, e=2))
+
         load(1, 1)
         load(2, 1)
-        vraw = const.tile([P, NH, 4, HD], BF16, name="vraw")
-        nc.sync.dma_start(out=vraw[:].rearrange("p g (u e) d -> p (g u) (e d)", u=2),
-                          in_=v_d.rearrange("b h (u p e) d -> p (b h u) (e d)", u=2, e=2))
+        vload(0)
         load(3, 1)
+        load(4, 1)
+        vload(1)
 
         tiles = [(m, t) for m in range(2) for t in range(T)]
 
-        def wk_on(h, e, maps=(0, 1)):
-            for m, t in tiles:
-                if m in maps and wk_engine(h, m, t) == e:
-                    wk(h, m, t)
-
         def head_rows(h, part):
-            for m, t in part:
-                rows(h, m, t, False)
+            if h < NH:
+                for m, t in part:
+                    rows(h, m, t, False)
 
         for t in range(T):
             rows(0, 0, t, t % 2 == 1)
-        head_rows(0, ((1, 0), (1, 1)))
-        recip(0, 0, 1)
-        root(0, 0, 1)
-        dbc(0, 0)
-        wk_on(0, "v", (0,))
-        head_rows(0, ((1, 2), (1, 3)))
-        head_rows(1, tiles[:1])
-        recip(0, 1, 2)
-        root(0, 1, 2)
-        dbc(0, 1)
-        cols(0, 0)
-        wk_on(0, "v", (1,))
-        wk_on(0, "s", (1,))
-        head_rows(1, tiles[1:])
+        head_rows(0, tiles[4:])
+        for m in range(2):
+            power(0, m, m + 1)
+            dbc(0, m)
+        head_rows(1, tiles)
         for b2 in range(2):
             turn(0, b2)
-        cols(0, 1)
+            turn_copy(0, b2)
+        scale(0, 0)
+        lace(0, 0, False)
+        scale(0, 1)
+        for i in range(T):
+            xturn(0, i)
+            xcopy(0, i)
+        lace(0, 1, True)
         for it in range(NH):
-            new = it + 3
-            scl = it + 2
             nxt = it + 1
+            two = it + 2
 
             def on(h):
                 return h < NH
 
-            if on(it + 4):
-                load(it + 4, 1)
-            if on(scl) and it > 0:
-                recip(scl)
-                root(scl)
+            if on(it + 5):
+                load(it + 5, 1)
             if it > 0:
                 q_a(it - 1)
             q_s(it)
             if it == 0:
-                recip(1)
                 gate(1)
-                for b2 in range(2):
-                    turn_copy(0, b2)
-                root(1)
-                wk_on(1, "g")
+                power(1)
+                dbc(1, 0)
                 for i in range(T):
-                    xturn(0, i)
-                    xcopy(0, i)
-                wk_on(1, "s")
+                    pmul(0, i)
+                vgroup(0, 0, NHB)
+                scale(1, 0)
                 head_rows(2, tiles)
-                vgroup(0)
+                head_rows(3, tiles[:4])
+            elif on(nxt):
+                gate(nxt)
             if on(nxt):
-                dbc(nxt, 0)
+                lace(nxt, 0, False)
+                dbc(nxt, 1)
             if it > 0:
+                for i in range(T):
+                    pmul(it, i)
                 if (it - 1) % NHB == 0:
                     q_v((it - 1) // NHB)
                 av(it - 1)
-            for i in range(T):
-                pmul(it, i)
-            if on(scl) and it > 0:
-                wk_on(scl, "v")
-                gate(scl)
-                wk_on(scl, "g")
+            head_rows(it + 3, tiles[4:])
             if it == 0:
-                for i in range(T):
-                    amix(0, i)
-                cols(1, 0)
-                recip(2)
-                gate(2)
-            if on(new):
-                head_rows(new, tiles[:5])
-            if it == 0:
-                root(2)
-                wk_on(2, "g")
+                power(2)
+            if on(nxt):
+                scale(nxt, 1)
+                lace(nxt, 1, False)
+            if on(it + 3):
+                power(it + 3)
             if it > 0:
                 ocopy(it - 1)
             if on(nxt):
-                if it > 0:
-                    cols(nxt, 0)
                 for b2 in range(2):
                     turn(nxt, b2)
+                for b2 in (1, 0):
                     turn_copy(nxt, b2)
-                dbc(nxt, 1)
-            if on(new):
-                head_rows(new, tiles[5:])
-            if on(scl):
-                wk_on(scl, "s")
+            if on(two):
+                dbc(two, 0)
+            head_rows(it + 4, tiles[:4])
+
+            if it == NH - 2:
+                for i in range(T):
+                    xturn(nxt, i)
+                    xcopy(nxt, i)
             if nxt == NH:
                 q_a(it, 0, N)
                 av(it, 0, T)
-            for i in range(T):
-                if it > 0:
-                    amix(it, i)
-                if on(nxt):
+            for i in (3, 0, 1, 2):
+                amix(it, i)
+            if it < NH - 2:
+                for i in (3, 0, 1, 2):
                     xturn(nxt, i)
+                for i in (2, 3, 0, 1):
                     xcopy(nxt, i)
-            if on(nxt):
-                cols(nxt, 1)
-            if it == NHB // 2:
-                vgroup(1)
+            if on(two):
+                scale(two, 0)
+            if 3 <= it < 7:
+                vgroup(1, 2 * it - 6, 2 * it - 4)
         ocopy(NH - 1, 0, T)
         for i in range(T, 2 * T, 2):
             q_a(NH - 1, P * i, P * i + 2 * P)

@@ -106,13 +106,12 @@ def tile_multiattention_pa_kernel(tc, attn_r, attn_d, v_d, out_rd, out_d):
         def lace(h, m, vector):
             s = st[h]
             if m == 0:
-                s["gs"] = sb.tile([P, 2, N, 4], BF16, name="gs", tag="gs", bufs=2, align_bytes=64)
+                s["gs"] = sb.tile([P, 2, N, 4], BF16, name="gs", tag="gs", bufs=1, align_bytes=64)
             src = s["sn%d" % m][:].rearrange("p t n -> p n t")
             if vector:
                 nc.vector.tensor_copy(out=s["gs"][:, m], in_=src)
             else:
-                add = s["zero"][:, 0:1] if m == 0 and "zero" in s else 0.0
-                nc.gpsimd.tensor_scalar(out=s["gs"][:, m], in0=src, scalar1=1.0, scalar2=add, op0=ALU.mult, op1=ALU.add)
+                nc.gpsimd.tensor_scalar(out=s["gs"][:, m], in0=src, scalar1=1.0, scalar2=0.0, op0=ALU.mult, op1=ALU.add)
 
         def quantise(h, src, tag, n0, n1):
             s = st[h]
@@ -198,11 +197,11 @@ def tile_multiattention_pa_kernel(tc, attn_r, attn_d, v_d, out_rd, out_d):
             b = h // NHB
             k = h % NHB
             q = k % 2
-            if q == 0 and b0 == 0:
+            last = h >= NH - 2
+            if b0 == 0 and (q == 0 or last):
                 st["o"] = sb.tile([P, 2 * T, 2 * HD], F32, name="o", tag="o", bufs=3)
             ot = st["o"]
             nc.scalar.copy(out=ot[:, b0:b1, HD * q:HD * q + HD], in_=st[h]["ob"][:, b0:b1, :])
-            last = h >= NH - 2
             if last or q == 1:
                 q0 = q if last else 0
                 c0 = HD * (k - q + q0)
@@ -217,8 +216,11 @@ def tile_multiattention_pa_kernel(tc, attn_r, attn_d, v_d, out_rd, out_d):
             if g0 == 0:
                 st["vg%d" % b] = sb.tile([P, NHB, HD, 4], BF16, name="vg", tag="vg", bufs=1, align_bytes=64)
             src = vraw[:, NHB * b + g0:NHB * b + g1].rearrange("p g j d -> p g d j")
-            add = st[1]["zero"][:, 0:1] if b == 0 else 0.0
-            nc.gpsimd.tensor_scalar(out=st["vg%d" % b][:, g0:g1], in0=src, scalar1=1.0, scalar2=add, op0=ALU.mult, op1=ALU.add)
+            out = st["vg%d" % b][:, g0:g1]
+            if b == 0:
+                nc.gpsimd.tensor_scalar(out=out, in0=src, scalar1=1.0, scalar2=st[1]["zero"][:, 0:1], op0=ALU.mult, op1=ALU.add)
+            else:
+                nc.scalar.copy(out=out, in_=src)
 
         def q_v(b):
             codes = sb.tile([P, NHB * HD], U32, name="cv", tag="cv", bufs=2, align_bytes=64)
@@ -252,9 +254,8 @@ def tile_multiattention_pa_kernel(tc, attn_r, attn_d, v_d, out_rd, out_d):
                 for m, t in part:
                     rows(h, m, t, False)
 
-        for t in range(T):
-            rows(0, 0, t, t % 2 == 1)
-        head_rows(0, tiles[4:])
+        for m, t in tiles:
+            rows(0, m, t, t % 2 == 1)
         for m in range(2):
             power(0, m, m + 1)
             dbc(0, m)
@@ -291,8 +292,6 @@ def tile_multiattention_pa_kernel(tc, attn_r, attn_d, v_d, out_rd, out_d):
                 scale(1, 0)
                 head_rows(2, tiles)
                 head_rows(3, tiles[:4])
-            elif on(nxt):
-                gate(nxt)
             if on(nxt):
                 lace(nxt, 0, False)
                 dbc(nxt, 1)
@@ -328,8 +327,10 @@ def tile_multiattention_pa_kernel(tc, attn_r, attn_d, v_d, out_rd, out_d):
             if nxt == NH:
                 q_a(it, 0, N)
                 av(it, 0, T)
-            for i in (3, 0, 1, 2):
+            for i in (3, 0, 1, 2) if 0 < it < NH - 1 else (0, 1, 2):
                 amix(it, i)
+            if it == 0:
+                amix(it, 3)
             if it < NH - 2:
                 for i in (3, 0, 1, 2):
                     xturn(nxt, i)
@@ -344,3 +345,5 @@ def tile_multiattention_pa_kernel(tc, attn_r, attn_d, v_d, out_rd, out_d):
             q_a(NH - 1, P * i, P * i + 2 * P)
             av(NH - 1, i, i + 2)
             ocopy(NH - 1, i, i + 2)
+            if i == T:
+                amix(NH - 1, 3)

@@ -76,6 +76,8 @@ def tile_multiattention_pa_kernel(tc, attn_r, attn_d, v_d, out_rd, out_d):
             s = st[h]
             if h == 0:
                 db = ps.tile([P, N], F32, name="dbc0", tag="pp", bufs=4)
+            elif (h, m) == (1, 1):
+                db = ps.tile([P, N], F32, name="dbc1", tag="tw", bufs=3)
             else:
                 db = ps.tile([P, N], F32, name="dbc", tag="dbc", bufs=1)
             for c in range(T):
@@ -85,7 +87,7 @@ def tile_multiattention_pa_kernel(tc, attn_r, attn_d, v_d, out_rd, out_d):
                 else:
                     out = db[:].rearrange("p (e r) -> p e r", e=2)[:, :, 64 * c:64 * c + 64]
                     eye = ident[:].rearrange("k (q e) -> k e q", e=2)
-                plain = h > 2 and T * m + c < PLAIN
+                plain = h > 1 and T * m + c < PLAIN
                 nc.tensor.matmul(out=out, lhsT=col, rhs=eye, is_transpose=not plain, start=True, stop=True)
             s["dbc%d" % m] = db
 
@@ -103,15 +105,16 @@ def tile_multiattention_pa_kernel(tc, attn_r, attn_d, v_d, out_rd, out_d):
                 nc.vector.scalar_tensor_tensor(out=dst, in0=src, scalar=s["d"][:, T * m + t:T * m + t + 1],
                                                in1=bc, op0=ALU.mult, op1=ALU.mult)
 
-        def lace(h, m, vector):
+        def lace(h, m, vector, n0=0, n1=N):
             s = st[h]
-            if m == 0:
+            if m == 0 and n0 == 0:
                 s["gs"] = sb.tile([P, 2, N, 4], BF16, name="gs", tag="gs", bufs=1, align_bytes=64)
-            src = s["sn%d" % m][:].rearrange("p t n -> p n t")
+            src = s["sn%d" % m][:].rearrange("p t n -> p n t")[:, n0:n1, :]
+            out = s["gs"][:, m, n0:n1, :]
             if vector:
-                nc.vector.tensor_copy(out=s["gs"][:, m], in_=src)
+                nc.vector.tensor_copy(out=out, in_=src)
             else:
-                nc.gpsimd.tensor_scalar(out=s["gs"][:, m], in0=src, scalar1=1.0, scalar2=0.0, op0=ALU.mult, op1=ALU.add)
+                nc.gpsimd.tensor_scalar(out=out, in0=src, scalar1=1.0, scalar2=0.0, op0=ALU.mult, op1=ALU.add)
 
         def quantise(h, src, tag, n0, n1):
             s = st[h]
@@ -154,7 +157,7 @@ def tile_multiattention_pa_kernel(tc, attn_r, attn_d, v_d, out_rd, out_d):
             for j in range(T):
                 for m in range(2):
                     nc.tensor.matmul(out=at[:, j, :], lhsT=s["x%d" % m][:, i, P * BLOCK[j]:P * BLOCK[j] + P], rhs=ident[:],
-                                     is_transpose=True, start=m == 0, stop=m == 1)
+                                     is_transpose=not (h == NH - 1 and j == 3), start=m == 0, stop=m == 1)
             s["at%d" % i] = at
 
         def xcopy(h, i):
@@ -264,11 +267,12 @@ def tile_multiattention_pa_kernel(tc, attn_r, attn_d, v_d, out_rd, out_d):
             turn(0, b2)
             turn_copy(0, b2)
         scale(0, 0)
-        lace(0, 0, False)
+        lace(0, 0, False, 0, 384)
         scale(0, 1)
         for i in range(T):
             xturn(0, i)
             xcopy(0, i)
+        lace(0, 0, True, 384, N)
         lace(0, 1, True)
         for it in range(NH):
             nxt = it + 1
@@ -286,6 +290,7 @@ def tile_multiattention_pa_kernel(tc, attn_r, attn_d, v_d, out_rd, out_d):
                 gate(1)
                 power(1)
                 dbc(1, 0)
+                dbc(1, 1)
                 for i in range(T):
                     pmul(0, i)
                 vgroup(0, 0, NHB)
@@ -294,7 +299,8 @@ def tile_multiattention_pa_kernel(tc, attn_r, attn_d, v_d, out_rd, out_d):
                 head_rows(3, tiles[:4])
             if on(nxt):
                 lace(nxt, 0, False)
-                dbc(nxt, 1)
+                if it > 0:
+                    dbc(nxt, 1)
             if it > 0:
                 for i in range(T):
                     pmul(it, i)

@@ -65,7 +65,7 @@ def tile_multiattention_pa_kernel(tc, attn_r, attn_d, v_d, out_rd, out_d):
             if m0 == 0:
                 s["d"] = sb.tile([P, 2 * T], F32, name="d", tag="d", bufs=3)
             w = slice(T * m0, T * m1)
-            nc.gpsimd.tensor_tensor(out=s["d"][:, w], in0=s["rs"][:, w], in1=mhalf[:, w], op=ALU.pow)
+            nc.scalar.activation(out=s["d"][:, w], in_=s["rs"][:, w], func=ACT.Abs_reciprocal_sqrt)
 
         def gate(h):
             s = st[h]
@@ -87,7 +87,7 @@ def tile_multiattention_pa_kernel(tc, attn_r, attn_d, v_d, out_rd, out_d):
                 else:
                     out = db[:].rearrange("p (e r) -> p e r", e=2)[:, :, 64 * c:64 * c + 64]
                     eye = ident[:].rearrange("k (q e) -> k e q", e=2)
-                plain = h > 1 and T * m + c < PLAIN
+                plain = (h > 2 or (h == 2 and m == 1)) and T * m + c < PLAIN
                 nc.tensor.matmul(out=out, lhsT=col, rhs=eye, is_transpose=not plain, start=True, stop=True)
             s["dbc%d" % m] = db
 
@@ -232,8 +232,10 @@ def tile_multiattention_pa_kernel(tc, attn_r, attn_d, v_d, out_rd, out_d):
                                   in_=st["vg%d" % b][:].rearrange("p g d j -> p (g d j)"))
             st["v%d" % b] = (codes, scales)
 
-        mhalf = const.tile([P, 2 * T], F32, name="mhalf")
-        nc.gpsimd.memset(mhalf[:], -0.5)
+        one = const.tile([P, 1], F32, name="one")
+        nc.vector.memset(one[:], 1.0)
+        warm = const.tile([P, 1], F32, name="warm")
+        nc.scalar.activation(out=warm[:], in_=one[:], func=ACT.Abs_reciprocal_sqrt)
         load(0, T)
         ident = const.tile([P, P], F32, name="ident")
         make_identity(nc, ident[:])
@@ -257,12 +259,16 @@ def tile_multiattention_pa_kernel(tc, attn_r, attn_d, v_d, out_rd, out_d):
                 for m, t in part:
                     rows(h, m, t, False)
 
-        for m, t in tiles:
+        for m, t in tiles[:6]:
             rows(0, m, t, t % 2 == 1)
-        for m in range(2):
-            power(0, m, m + 1)
-            dbc(0, m)
+        power(0, 0, 1)
+        dbc(0, 0)
+        for m, t in tiles[6:]:
+            rows(0, m, t, t % 2 == 1)
+        power(0, 1, 2)
+        dbc(0, 1)
         head_rows(1, tiles)
+        power(1)
         for b2 in range(2):
             turn(0, b2)
             turn_copy(0, b2)
@@ -288,7 +294,6 @@ def tile_multiattention_pa_kernel(tc, attn_r, attn_d, v_d, out_rd, out_d):
             q_s(it)
             if it == 0:
                 gate(1)
-                power(1)
                 dbc(1, 0)
                 dbc(1, 1)
                 for i in range(T):
@@ -296,6 +301,7 @@ def tile_multiattention_pa_kernel(tc, attn_r, attn_d, v_d, out_rd, out_d):
                 vgroup(0, 0, NHB)
                 scale(1, 0)
                 head_rows(2, tiles)
+                power(2)
                 head_rows(3, tiles[:4])
             if on(nxt):
                 lace(nxt, 0, False)
@@ -308,13 +314,11 @@ def tile_multiattention_pa_kernel(tc, attn_r, attn_d, v_d, out_rd, out_d):
                     q_v((it - 1) // NHB)
                 av(it - 1)
             head_rows(it + 3, tiles[4:])
-            if it == 0:
-                power(2)
+            if on(it + 3):
+                power(it + 3)
             if on(nxt):
                 scale(nxt, 1)
                 lace(nxt, 1, False)
-            if on(it + 3):
-                power(it + 3)
             if it > 0:
                 ocopy(it - 1)
             if on(nxt):
@@ -324,7 +328,6 @@ def tile_multiattention_pa_kernel(tc, attn_r, attn_d, v_d, out_rd, out_d):
                     turn_copy(nxt, b2)
             if on(two):
                 dbc(two, 0)
-            head_rows(it + 4, tiles[:4])
 
             if it == NH - 2:
                 for i in range(T):
@@ -342,6 +345,7 @@ def tile_multiattention_pa_kernel(tc, attn_r, attn_d, v_d, out_rd, out_d):
                     xturn(nxt, i)
                 for i in (2, 3, 0, 1):
                     xcopy(nxt, i)
+            head_rows(it + 4, tiles[:4])
             if on(two):
                 scale(two, 0)
             if 3 <= it < 7:

from contextlib import ExitStack

import concourse.mybir as mybir
from concourse.masks import make_identity

F32 = mybir.dt.float32
BF16 = mybir.dt.bfloat16
U32 = mybir.dt.uint32
U8 = mybir.dt.uint8
FP8X4 = mybir.dt.float8_e4m3fn_x4
ALU = mybir.AluOpType
ACT = mybir.ActivationFunctionType

P = 128
N = 512
T = N // P
HD = 64
NHB = 8
NH = 16
ALPHA = 0.6
BETA = 0.4

FLOPS = NH * (2 * N * N * N + 2 * 2 * N * N * HD)

BLOCK = (0, 2, 1, 3)
PLAIN = 7


def tile_multiattention_pa_kernel(tc, attn_r, attn_d, v_d, out_rd, out_d):
    nc = tc.nc
    maps = [a.rearrange("b h (t p) n -> (b h) p t n", p=P) for a in (attn_r, attn_d)]
    with ExitStack() as ctx:
        const = ctx.enter_context(tc.tile_pool(name="const", bufs=1))
        sb = ctx.enter_context(tc.tile_pool(name="sb", bufs=2))
        ps = ctx.enter_context(tc.psum_pool(name="ps", bufs=1))
        ctx.enter_context(tc.manual_schedule())

        st = {}

        def load(h, pieces):
            s = {}
            st[h] = s
            w = T // pieces
            for m in range(2):
                s["n%d" % m] = sb.tile([P, T, N], BF16, name="n%d" % m, tag="n%d" % m, bufs=5 + m)
                for c in range(pieces):
                    nc.sync.dma_start(out=s["n%d" % m][:, w * c:w * c + w, :], in_=maps[m][h][:, w * c:w * c + w, :])

        def rows(h, m, t, vector):
            s = st[h]
            if m == 0 and t == 0:
                s["x0"] = sb.tile([P, T, N], F32, name="x0", tag="x0", bufs=4)
                s["x1"] = sb.tile([P, T, N], F32, name="x1", tag="x1", bufs=4)
                s["rs"] = sb.tile([P, 2 * T], F32, name="rs", tag="rs", bufs=3)
            src = s["n%d" % m][:, t, :].rearrange("p (r e) -> p e r", e=2)
            dst = s["x%d" % m][:, t, :].rearrange("p (e r) -> p e r", e=2)
            acc = s["rs"][:, T * m + t:T * m + t + 1]
            if vector:
                nc.vector.tensor_scalar(out=dst, in0=src, scalar1=1.0, scalar2=0.0, op0=ALU.mult, op1=ALU.add, accum_out=acc)
            else:
                nc.scalar.activation(out=dst, in_=src, func=ACT.Copy, accum_out=acc)

        def power(h, m0=0, m1=2):
            s = st[h]
            if m0 == 0:
                s["d"] = sb.tile([P, 2 * T], F32, name="d", tag="d", bufs=3)
            w = slice(T * m0, T * m1)
            nc.scalar.activation(out=s["d"][:, w], in_=s["rs"][:, w], func=ACT.Abs_reciprocal_sqrt)

        def gate(h):
            s = st[h]
            s["zero"] = sb.tile([P, 2], F32, name="zero", tag="zero")
            nc.vector.memset(s["zero"][:], 0.0)

        def dbc(h, m):
            s = st[h]
            if h == 0:
                db = ps.tile([P, N], F32, name="dbc0", tag="pp", bufs=4)
            elif (h, m) == (1, 1):
                db = ps.tile([P, N], F32, name="dbc1", tag="tw", bufs=3)
            else:
                db = ps.tile([P, N], F32, name="dbc", tag="dbc", bufs=1)
            for c in range(T):
                col = s["d"][:, T * m + c:T * m + c + 1].to_broadcast([P, P])
                if m == 0:
                    out, eye = db[:, P * c:P * c + P], ident[:]
                else:
                    out = db[:].rearrange("p (e r) -> p e r", e=2)[:, :, 64 * c:64 * c + 64]
                    eye = ident[:].rearrange("k (q e) -> k e q", e=2)
                plain = (h > 2 or (h == 2 and m == 1)) and T * m + c < PLAIN
                nc.tensor.matmul(out=out, lhsT=col, rhs=eye, is_transpose=not plain, start=True, stop=True)
            s["dbc%d" % m] = db

        def scale(h, m):
            s = st[h]
            s["sn%d" % m] = sb.tile([P, T, N], BF16, name="sn%d" % m, tag="sn%d" % m, bufs=2)
            for t in range(T):
                src = s["n%d" % m][:, t, :]
                dst = s["sn%d" % m][:, t, :]
                bc = s["dbc%d" % m][:]
                if m == 1:
                    src = src.rearrange("p (r e) -> p e r", e=2)
                    dst = dst.rearrange("p (e r) -> p e r", e=2)
                    bc = bc.rearrange("p (e r) -> p e r", e=2)
                nc.vector.scalar_tensor_tensor(out=dst, in0=src, scalar=s["d"][:, T * m + t:T * m + t + 1],
                                               in1=bc, op0=ALU.mult, op1=ALU.mult)

        def lace(h, m, vector, n0=0, n1=N):
            s = st[h]
            if m == 0 and n0 == 0:
                s["gs"] = sb.tile([P, 2, N, 4], BF16, name="gs", tag="gs", bufs=1, align_bytes=64)
            src = s["sn%d" % m][:].rearrange("p t n -> p n t")[:, n0:n1, :]
            out = s["gs"][:, m, n0:n1, :]
            if vector:
                nc.vector.tensor_copy(out=out, in_=src)
            else:
                nc.gpsimd.tensor_scalar(out=out, in0=src, scalar1=1.0, scalar2=0.0, op0=ALU.mult, op1=ALU.add)

        def quantise(h, src, tag, n0, n1):
            s = st[h]
            if n0 == 0:
                codes = sb.tile([P, 2 * N], U32, name="c" + tag, tag="c" + tag, bufs=2, align_bytes=64)
                scales = sb.tile([P, 2 * N], U8, name="s" + tag, tag="s" + tag, bufs=2, align_bytes=64)
                s["c" + tag] = (codes, scales)
            codes, scales = s["c" + tag]
            nc.vector.quantize_mx(
                out=codes[:, n0:n1].bitcast(FP8X4),
                scales=scales[:, n0:n1],
                in_=src[:].rearrange("p a n t -> p (a n t)")[:, 4 * n0:4 * n1])

        def q_s(h):
            quantise(h, st[h]["gs"], "s", 0, 2 * N)

        def q_a(h, n0=0, n1=2 * N):
            quantise(h, st[h]["gaw"], "a", n0, n1)

        def pmul(h, i):
            s = st[h]
            codes, scales = s["cs"]
            pp = ps.tile([P, T, P], F32, name="pp", tag="pp", bufs=4)
            for j in range(T):
                d0 = N + P * BLOCK[j]
                nc.tensor.matmul_mx(out=pp[:, j, :], lhsT=codes[:, d0:d0 + P].bitcast(FP8X4), lhsT_scale=scales[:, d0:d0 + P],
                                    rhs=codes[:, P * i:P * i + P].bitcast(FP8X4), rhs_scale=scales[:, P * i:P * i + P],
                                    start=True, stop=True)
            s["pp%d" % i] = pp

        def amix(h, i):
            s = st[h]
            nc.vector.scalar_tensor_tensor(out=s["gaw"][:, 1, P * i:P * i + P, :],
                                           in0=s["pp%d" % i][:].rearrange("p j n -> p n j"), scalar=ALPHA,
                                           in1=s["xt"][:, P * i:P * i + P, :], op0=ALU.mult, op1=ALU.add)

        def xturn(h, i):
            s = st[h]
            at = ps.tile([P, T, P], F32, name="at", tag="tw" if h == NH - 1 else "pp", bufs=3 if h == NH - 1 else 4)
            for j in range(T):
                for m in range(2):
                    nc.tensor.matmul(out=at[:, j, :], lhsT=s["x%d" % m][:, i, P * BLOCK[j]:P * BLOCK[j] + P], rhs=ident[:],
                                     is_transpose=not (h == NH - 1 and j == 3), start=m == 0, stop=m == 1)
            s["at%d" % i] = at

        def xcopy(h, i):
            s = st[h]
            if "xt" not in s:
                s["xt"] = sb.tile([P, N, T], F32, name="xt", tag="xt", bufs=3)
            out, in_ = s["xt"][:, P * i:P * i + P, :], s["at%d" % i][:].rearrange("p j n -> p n j")
            nc.scalar.activation(out=out, in_=in_, func=ACT.Copy, scale=BETA)

        def turn(h, b2):
            s = st[h]
            if b2 == 0:
                s["gaw"] = sb.tile([P, 2, N, 4], BF16, name="gaw", tag="gaw", bufs=2, align_bytes=64)
            words = s["n1"][:].bitcast(F32)
            tw = ps.tile([P, 2, 256], F32, name="tw", tag="tw", bufs=3)
            for ii in range(2):
                for u in range(2):
                    nc.tensor.transpose(tw[:, u, P * ii:P * ii + P], words[:, 2 * b2 + ii, P * u:P * u + P], ident[:])
            s["tw%d" % b2] = tw

        def turn_copy(h, b2):
            s = st[h]
            g32 = s["gaw"][:, 0].bitcast(F32)
            nc.scalar.copy(out=g32[:, 256 * b2:256 * b2 + 256, :], in_=s["tw%d" % b2][:].rearrange("p u n -> p n u"))

        def av(h, b0=0, b1=2 * T):
            s = st[h]
            codes, scales = s["ca"]
            c0 = HD * (h % NHB)
            vc, vs = st["v%d" % (h // NHB)]
            if b0 == 0:
                s["ob"] = ps.tile([P, 2 * T, HD], F32, name="ob", tag="tw", bufs=3)
            for i in range(b0, b1):
                nc.tensor.matmul_mx(out=s["ob"][:, i, :], lhsT=codes[:, P * i:P * i + P].bitcast(FP8X4),
                                    lhsT_scale=scales[:, P * i:P * i + P],
                                    rhs=vc[:, c0:c0 + HD].bitcast(FP8X4), rhs_scale=vs[:, c0:c0 + HD],
                                    start=True, stop=True)

        def ocopy(h, b0=0, b1=2 * T):
            b = h // NHB
            k = h % NHB
            q = k % 2
            last = h >= NH - 2
            if b0 == 0 and (q == 0 or last):
                st["o"] = sb.tile([P, 2 * T, 2 * HD], F32, name="o", tag="o", bufs=3)
            ot = st["o"]
            nc.scalar.copy(out=ot[:, b0:b1, HD * q:HD * q + HD], in_=st[h]["ob"][:, b0:b1, :])
            if last or q == 1:
                q0 = q if last else 0
                c0 = HD * (k - q + q0)
                w = HD * (q + 1 - q0)
                for o, dst in enumerate((out_d, out_rd)):
                    i0, i1 = max(b0, T * o), min(b1, T * o + T)
                    if i0 < i1:
                        nc.sync.dma_start(out=dst[b].rearrange("(i p) c -> p i c", p=P)[:, i0 - T * o:i1 - T * o, c0:c0 + w],
                                          in_=ot[:, i0:i1, HD * q0:HD * q0 + w])

        def vgroup(b, g0, g1):
            if g0 == 0:
                st["vg%d" % b] = sb.tile([P, NHB, HD, 4], BF16, name="vg", tag="vg", bufs=1, align_bytes=64)
            src = vraw[:, NHB * b + g0:NHB * b + g1].rearrange("p g j d -> p g d j")
            out = st["vg%d" % b][:, g0:g1]
            if b == 0:
                nc.gpsimd.tensor_scalar(out=out, in0=src, scalar1=1.0, scalar2=st[1]["zero"][:, 0:1], op0=ALU.mult, op1=ALU.add)
            else:
                nc.scalar.copy(out=out, in_=src)

        def q_v(b):
            codes = sb.tile([P, NHB * HD], U32, name="cv", tag="cv", bufs=2, align_bytes=64)
            scales = sb.tile([P, NHB * HD], U8, name="sv", tag="sv", bufs=2, align_bytes=64)
            nc.vector.quantize_mx(out=codes[:].bitcast(FP8X4), scales=scales[:],
                                  in_=st["vg%d" % b][:].rearrange("p g d j -> p (g d j)"))
            st["v%d" % b] = (codes, scales)

        one = const.tile([P, 1], F32, name="one")
        nc.vector.memset(one[:], 1.0)
        warm = const.tile([P, 1], F32, name="warm")
        nc.scalar.activation(out=warm[:], in_=one[:], func=ACT.Abs_reciprocal_sqrt)
        load(0, T)
        ident = const.tile([P, P], F32, name="ident")
        make_identity(nc, ident[:])
        vraw = const.tile([P, NH, 4, HD], BF16, name="vraw")

        def vload(b):
            nc.sync.dma_start(out=vraw[:, NHB * b:NHB * b + NHB].rearrange("p g (u e) d -> p (g u) (e d)", u=2),
                              in_=v_d[b].rearrange("h (u p e) d -> p (h u) (e d)", u=2, e=2))

        load(1, 1)
        load(2, 1)
        vload(0)
        load(3, 1)
        load(4, 1)
        vload(1)

        tiles = [(m, t) for m in range(2) for t in range(T)]

        def head_rows(h, part):
            if h < NH:
                for m, t in part:
                    rows(h, m, t, False)

        for m, t in tiles[:6]:
            rows(0, m, t, t % 2 == 1)
        power(0, 0, 1)
        dbc(0, 0)
        for m, t in tiles[6:]:
            rows(0, m, t, t % 2 == 1)
        power(0, 1, 2)
        dbc(0, 1)
        head_rows(1, tiles)
        power(1)
        for b2 in range(2):
            turn(0, b2)
            turn_copy(0, b2)
        scale(0, 0)
        lace(0, 0, False, 0, 384)
        scale(0, 1)
        for i in range(T):
            xturn(0, i)
            xcopy(0, i)
        lace(0, 0, True, 384, N)
        lace(0, 1, True)
        for it in range(NH):
            nxt = it + 1
            two = it + 2

            def on(h):
                return h < NH

            if on(it + 5):
                load(it + 5, 1)
            if it > 0:
                q_a(it - 1)
            q_s(it)
            if it == 0:
                gate(1)
                dbc(1, 0)
                dbc(1, 1)
                for i in range(T):
                    pmul(0, i)
                vgroup(0, 0, NHB)
                scale(1, 0)
                head_rows(2, tiles)
                power(2)
                head_rows(3, tiles[:4])
            if on(nxt):
                lace(nxt, 0, False)
                if it > 0:
                    dbc(nxt, 1)
            if it > 0:
                for i in range(T):
                    pmul(it, i)
                if (it - 1) % NHB == 0:
                    q_v((it - 1) // NHB)
                av(it - 1)
            head_rows(it + 3, tiles[4:])
            if on(it + 3):
                power(it + 3)
            if on(nxt):
                scale(nxt, 1)
                lace(nxt, 1, False)
            if it > 0:
                ocopy(it - 1)
            if on(nxt):
                for b2 in range(2):
                    turn(nxt, b2)
                for b2 in (1, 0):
                    turn_copy(nxt, b2)
            if on(two):
                dbc(two, 0)

            if it == NH - 2:
                for i in range(T):
                    xturn(nxt, i)
                    xcopy(nxt, i)
            if nxt == NH:
                q_a(it, 0, N)
                av(it, 0, T)
            for i in (3, 0, 1, 2) if 0 < it < NH - 1 else (0, 1, 2):
                amix(it, i)
            if it == 0:
                amix(it, 3)
            if it < NH - 2:
                for i in (3, 0, 1, 2):
                    xturn(nxt, i)
                for i in (2, 3, 0, 1):
                    xcopy(nxt, i)
            head_rows(it + 4, tiles[:4])
            if on(two):
                scale(two, 0)
            if 3 <= it < 7:
                vgroup(1, 2 * it - 6, 2 * it - 4)
        ocopy(NH - 1, 0, T)
        for i in range(T, 2 * T, 2):
            q_a(NH - 1, P * i, P * i + 2 * P)
            av(NH - 1, i, i + 2)
            ocopy(NH - 1, i, i + 2)
            if i == T:
                amix(NH - 1, 3)
